import numpy as np
import ml_dtypes


def mxq(x, axis, fmt="e4m3"):
    dtype, down = {"e4m3": (ml_dtypes.float8_e4m3fn, 7), "e5m2": (ml_dtypes.float8_e5m2, 14)}[fmt]
    v = np.moveaxis(np.asarray(x, np.float32).astype(ml_dtypes.bfloat16).astype(np.float64), axis, -1)
    blocks = v.reshape(v.shape[:-1] + (-1, 32))
    amax = np.abs(blocks).max(-1, keepdims=True)
    byte = np.maximum(np.where(amax > 0, np.frexp(amax)[1] - 1 + 127, 0) - down, 1)
    scale = np.exp2(byte - 127.0)
    codes = (blocks / scale).astype(np.float32).astype(dtype).astype(np.float64)
    return np.moveaxis((codes * scale).reshape(v.shape), -1, axis)


WIDE = False


def mx_kscale(k):
    if not WIDE:
        return np.ones(k)
    levels = np.array([10, -10, 5, -5, 0])
    if k % 512:
        return np.exp2(np.random.permutation(np.resize(levels, k // 32))).repeat(32)
    a = np.empty((k // 512, 16))
    for p in range(k // 512):
        a[p, :8] = np.random.permutation(np.resize(levels, 8))
        for g in range(8):
            far = levels[np.abs(levels - a[p, g]) >= 10]
            a[p, g + 8] = far[np.random.randint(len(far))]
    return np.exp2(a.ravel()).repeat(32)


BF16 = ml_dtypes.bfloat16


def bf(x):
    return np.asarray(x, np.float32).astype(BF16)


def f64(x):
    return np.asarray(x).astype(np.float64)


B, CH, C1, C2, D, NF, W, H = 2, 1024, 128, 256, 2, 16, 16, 16
N = NF * W * H
M = NF * (W // D) * (H // D)


def conv(xq, w, b):
    return (mxq(f64(w), 1, "e4m3") @ xq) + f64(b)[None, :, None]


def maxpool_wh(v):
    return v.reshape(B, -1, NF, W // D, D, H // D, D).max(axis=(4, 6)).reshape(B, -1, M)


def setup_inputs():
    s = mx_kscale(CH)
    return {"x": bf(np.random.standard_normal((B, CH, NF, W, H)) * s[None, :, None, None, None]),
            "w_theta": bf(np.random.standard_normal((C1, CH)) * 0.3 / np.sqrt(CH) / s),
            "b_theta": bf(np.random.standard_normal(C1) * 0.1),
            "w_phi": bf(np.random.standard_normal((C1, CH)) * 0.3 / np.sqrt(CH) / s),
            "b_phi": bf(np.random.standard_normal(C1) * 0.1),
            "w_g": bf(np.random.standard_normal((C2, CH)) / np.sqrt(CH) / s),
            "b_g": bf(np.random.standard_normal(C2) * 0.2)}


def reference(x, w_theta, b_theta, w_phi, b_phi, w_g, b_g):
    xq = mxq(f64(x).reshape(B, CH, N), 1, "e4m3")
    theta = np.tanh(conv(xq, w_theta, b_theta)).transpose(0, 2, 1)
    phi = maxpool_wh(np.tanh(conv(xq, w_phi, b_phi))).transpose(0, 2, 1)
    g = maxpool_wh(conv(xq, w_g, b_g)).transpose(0, 2, 1)
    return theta, phi, g

@@ -1,0 +1,256 @@
+from contextlib import ExitStack
+
+import concourse.mybir as mybir
+from concourse.masks import make_identity
+
+BF16 = mybir.dt.bfloat16
+F32 = mybir.dt.float32
+U32 = mybir.dt.uint32
+U8 = mybir.dt.uint8
+FP8X4 = mybir.dt.float8_e4m3fn_x4
+ACT = mybir.ActivationFunctionType
+
+P = 128
+PACK = 4
+K_PASS = P * PACK
+BATCH = 2
+CH = 1024
+PASSES = CH // K_PASS
+LOCS = 16 * 16 * 16
+SLAB = 1024
+CHUNK = 512
+SLABS_PER_BATCH = LOCS // SLAB
+X_TILES = BATCH * SLABS_PER_BATCH * PASSES
+CHUNKS = BATCH * LOCS // CHUNK
+OUT_TILES = 4
+POOLED_TILES = 3
+THETA = 3
+POOLED = SLAB // 4
+V_COLS = 360
+G_COLS = 256
+
+LOADS_AHEAD = 6
+
+FLOPS = 2 * BATCH * LOCS * CH * OUT_TILES * P
+
+
+def tile_selfattention3d_pb_t_kernel(
+    tc, x, w_theta, b_theta, w_phi, b_phi, w_g, b_g, out_0, out_1, out_2
+):
+    nc = tc.nc
+    x_view = x.rearrange("b (g p t) f i j -> b g p t (f i j)", g=PASSES, t=PACK, p=P)
+
+    with ExitStack() as ctx:
+        consts = ctx.enter_context(tc.tile_pool(name="consts", bufs=1))
+        raw_pool = ctx.enter_context(tc.tile_pool(name="raw", bufs=6))
+        grouped_pool = ctx.enter_context(tc.tile_pool(name="grouped", bufs=3))
+        mx_pool = ctx.enter_context(tc.tile_pool(name="mx", bufs=6))
+        work = ctx.enter_context(tc.tile_pool(name="work", bufs=3))
+        psum_acc = ctx.enter_context(tc.psum_pool(name="psum_acc", bufs=5))
+        psum_tr = ctx.enter_context(tc.psum_pool(name="psum_tr", bufs=3))
+
+        raw = {}
+        grouped = {}
+        x_codes = {}
+        x_scales = {}
+        theta_act = {}
+        pooled = {}
+        pooled_act = {}
+
+        def load(j):
+            s, g = j // PASSES, j % PASSES
+            bt, n0 = s // SLABS_PER_BATCH, (s % SLABS_PER_BATCH) * SLAB
+            rows = raw_pool.tile([P, PACK, SLAB], BF16)
+            nc.sync.dma_start(out=rows[:], in_=x_view[bt, g, :, :, n0 : n0 + SLAB])
+            raw[j] = rows
+
+        def regroup(j):
+            quads = grouped_pool.tile([P, SLAB, PACK], BF16, align_bytes=64)
+            dst = quads[:].rearrange("p (c i) t -> p c t i", i=4)
+            src = raw[j][:].rearrange("p t (c i) -> p c t i", i=4)
+            v_end = V_COLS // 4
+            g_end = (V_COLS + G_COLS) // 4
+            nc.vector.tensor_copy(out=dst[:, :v_end], in_=src[:, :v_end])
+            nc.gpsimd.tensor_scalar(
+                out=dst[:, v_end:g_end],
+                in0=src[:, v_end:g_end],
+                scalar1=1.0,
+                scalar2=0.0,
+                op0=mybir.AluOpType.mult,
+                op1=mybir.AluOpType.add,
+            )
+            nc.scalar.copy(out=dst[:, g_end:], in_=src[:, g_end:])
+            grouped[j] = quads
+
+        def quantise(j):
+            codes = mx_pool.tile([P, SLAB], U32, align_bytes=64)
+            scales = mx_pool.tile([P, SLAB], U8, align_bytes=64)
+            nc.vector.quantize_mx(
+                out=codes[:].bitcast(FP8X4),
+                scales=scales[:],
+                in_=grouped[j][:].rearrange("p n t -> p (n t)"),
+            )
+            x_codes[j] = codes
+            x_scales[j] = scales
+
+        def convolve(s, u):
+            cols = slice(u * CHUNK, (u + 1) * CHUNK)
+            if u == 0:
+                pooled[s] = work.tile([P, POOLED_TILES, POOLED], F32, name="pooled_max")
+            for o in range(OUT_TILES):
+                outs = slice(o * P, (o + 1) * P)
+                acc = psum_acc.tile([P, CHUNK], F32)
+                for g in range(PASSES):
+                    nc.tensor.matmul_mx(
+                        out=acc[:],
+                        lhsT=w_codes[:, g, outs].bitcast(FP8X4),
+                        lhsT_scale=w_scales[:, g, outs],
+                        rhs=x_codes[PASSES * s + g][:, cols].bitcast(FP8X4),
+                        rhs_scale=x_scales[PASSES * s + g][:, cols],
+                        start=(g == 0),
+                        stop=(g == PASSES - 1),
+                    )
+                if o < POOLED_TILES:
+                    nc.vector.tensor_reduce(
+                        out=pooled[s][:, o, u * P : (u + 1) * P].rearrange(
+                            "p (r j) -> p r j", j=8
+                        ),
+                        in_=acc[:].rearrange("p (r a j b) -> p r j a b", a=2, j=8, b=2),
+                        axis=mybir.AxisListType.XY,
+                        op=mybir.AluOpType.max,
+                    )
+                else:
+                    th = work.tile([P, 4, P], F32, name="th")
+                    nc.scalar.activation(
+                        out=th[:],
+                        in_=acc[:].rearrange("p (q r) -> p r q", r=4),
+                        func=ACT.Tanh,
+                        bias=bias_col[:, THETA : THETA + 1],
+                    )
+                    theta_act[(s, u)] = th
+
+        def store_theta(s, u):
+            bt = s // SLABS_PER_BATCH
+            n0 = (s % SLABS_PER_BATCH) * SLAB + u * CHUNK
+            th_t = psum_tr.tile([P, 4, P], F32, tag="tr")
+            for r in range(4):
+                nc.tensor.transpose(th_t[:, r, :], theta_act[(s, u)][:, r, :], ident_f32[:])
+            th_out = work.tile([P, 4, P], F32)
+            nc.scalar.copy(out=th_out[:], in_=th_t[:])
+            nc.sync.dma_start(
+                out=out_0[bt, n0 : n0 + CHUNK, :].rearrange("(q r) c -> q r c", r=4),
+                in_=th_out[:],
+            )
+
+        def activate_pooled(s):
+            acted = work.tile([P, POOLED_TILES, 2, P], F32)
+            for o in range(POOLED_TILES):
+                nc.scalar.activation(
+                    out=acted[:, o, :, :],
+                    in_=pooled[s][:, o, :].rearrange("p (q r) -> p r q", r=2),
+                    func=(ACT.Tanh if o == 0 else ACT.Identity),
+                    bias=bias_col[:, o : o + 1],
+                )
+            pooled_act[s] = acted
+
+        def store_pooled(s):
+            bt = s // SLABS_PER_BATCH
+            m0 = (s % SLABS_PER_BATCH) * POOLED
+            phi_t = psum_tr.tile([P, 2, P], F32, tag="tr")
+            g_t = psum_tr.tile([P, 2, 2, P], F32, tag="tr")
+            for r in range(2):
+                nc.tensor.transpose(phi_t[:, r, :], pooled_act[s][:, 0, r, :], ident_f32[:])
+                for h in range(2):
+                    nc.tensor.transpose(
+                        g_t[:, r, h, :], pooled_act[s][:, 1 + h, r, :], ident_f32[:]
+                    )
+            phi_out = work.tile([P, 2, P], F32)
+            nc.scalar.copy(out=phi_out[:], in_=phi_t[:])
+            g_out = work.tile([P, 2, 2 * P], F32)
+            nc.scalar.copy(out=g_out[:], in_=g_t[:].rearrange("p r h c -> p r (h c)"))
+            nc.sync.dma_start(
+                out=out_1[bt, m0 : m0 + POOLED, :].rearrange("(q r) c -> q r c", r=2),
+                in_=phi_out[:],
+            )
+            nc.sync.dma_start(
+                out=out_2[bt, m0 : m0 + POOLED, :].rearrange("(q r) c -> q r c", r=2),
+                in_=g_out[:],
+            )
+
+        load(0)
+        load(1)
+        w_rows = consts.tile([P, OUT_TILES, CH], BF16)
+        nc.sync.dma_start(out=w_rows[:, 0, :], in_=w_phi)
+        nc.sync.dma_start(out=w_rows[:, 1:3, :], in_=w_g.rearrange("(h o) k -> o h k", h=2))
+        nc.sync.dma_start(out=w_rows[:, THETA, :], in_=w_theta)
+        for j in range(2, LOADS_AHEAD):
+            load(j)
+
+        bias_rows = consts.tile([P, P], BF16)
+        nc.vector.memset(bias_rows[:], 0.0)
+        nc.scalar.dma_start(out=bias_rows[0:1, :], in_=b_phi.rearrange("(h c) -> h c", h=1))
+        nc.scalar.dma_start(out=bias_rows[1:3, :], in_=b_g.rearrange("(h c) -> h c", h=2))
+        nc.scalar.dma_start(
+            out=bias_rows[THETA : THETA + 1, :], in_=b_theta.rearrange("(h c) -> h c", h=1)
+        )
+        ident_bf = consts.tile([P, P], BF16)
+        make_identity(nc, ident_bf[:])
+        ident_f32 = consts.tile([P, P], F32)
+        make_identity(nc, ident_f32[:])
+
+        regroup(0)
+        regroup(1)
+
+        w_grouped = consts.tile([P, PASSES, OUT_TILES * P, PACK], BF16, align_bytes=64)
+        w_codes = consts.tile([P, PASSES, OUT_TILES * P], U32, align_bytes=64)
+        w_scales = consts.tile([P, PASSES, OUT_TILES * P], U8, align_bytes=64)
+        w_words = w_rows[:].bitcast(F32)
+        w_grouped_words = w_grouped[:].bitcast(F32)
+        for g in range(PASSES):
+            for h in range(2):
+                w_t = psum_tr.tile([P, 2, 2, P], F32, tag="tr")
+                for o in range(2):
+                    for u in range(2):
+                        w0 = g * (K_PASS // 2)
+                        nc.tensor.transpose(
+                            w_t[:, o, u, :],
+                            w_words[:, 2 * h + o, w0 + u : w0 + K_PASS // 2 : 2],
+                            ident_f32[:],
+                        )
+                dst = w_grouped_words[:, g, 2 * h * P : (2 * h + 2) * P, :].rearrange(
+                    "p (o r) u -> p o r u", o=2
+                )
+                src = w_t[:].rearrange("p o u r -> p o r u")
+                if h == 0:
+                    nc.vector.tensor_copy(out=dst, in_=src)
+                else:
+                    nc.scalar.copy(out=dst, in_=src)
+        bias_t = psum_tr.tile([P, P], BF16, tag="tr")
+        nc.tensor.transpose(bias_t[:], bias_rows[:], ident_bf[:])
+        bias_col = consts.tile([P, OUT_TILES], F32)
+        nc.vector.tensor_copy(out=bias_col[:], in_=bias_t[:, 0:OUT_TILES])
+        for g in range(PASSES):
+            nc.vector.quantize_mx(
+                out=w_codes[:, g, :].bitcast(FP8X4),
+                scales=w_scales[:, g, :],
+                in_=w_grouped[:, g, :, :].rearrange("p r t -> p (r t)"),
+            )
+        quantise(0)
+        regroup(2)
+        quantise(1)
+
+        for h in range(CHUNKS + 1):
+            if h + LOADS_AHEAD < X_TILES:
+                load(h + LOADS_AHEAD)
+            if h + 3 < X_TILES:
+                regroup(h + 3)
+            if h + 2 < X_TILES:
+                quantise(h + 2)
+            if h < CHUNKS:
+                convolve(h // 2, h % 2)
+            if h > 0:
+                store_theta((h - 1) // 2, (h - 1) % 2)
+                if h % 2 == 0:
+                    store_pooled((h - 1) // 2)
+            if h % 2 == 1:
+                activate_pooled(h // 2)

@@ -26,8 +26,8 @@ OUT_TILES = 4
 POOLED_TILES = 3
 THETA = 3
 POOLED = SLAB // 4
-V_COLS = 360
-G_COLS = 256
+V_COLS = 160
+G_COLS = 384
 
 LOADS_AHEAD = 6
 
@@ -55,7 +55,7 @@ def tile_selfattention3d_pb_t_kernel(
         x_scales = {}
         theta_act = {}
         pooled = {}
-        pooled_act = {}
+        phi_act = {}
 
         def load(j):
             s, g = j // PASSES, j % PASSES
@@ -72,8 +72,8 @@ def tile_selfattention3d_pb_t_kernel(
             g_end = (V_COLS + G_COLS) // 4
             nc.vector.tensor_copy(out=dst[:, :v_end], in_=src[:, :v_end])
             nc.gpsimd.tensor_scalar(
-                out=dst[:, v_end:g_end],
-                in0=src[:, v_end:g_end],
+                out=quads[:, V_COLS : V_COLS + G_COLS, :],
+                in0=raw[j][:, :, V_COLS : V_COLS + G_COLS].rearrange("p t n -> p n t"),
                 scalar1=1.0,
                 scalar2=0.0,
                 op0=mybir.AluOpType.mult,
@@ -142,16 +142,15 @@ def tile_selfattention3d_pb_t_kernel(
                 in_=th_out[:],
             )
 
-        def activate_pooled(s):
-            acted = work.tile([P, POOLED_TILES, 2, P], F32)
-            for o in range(POOLED_TILES):
-                nc.scalar.activation(
-                    out=acted[:, o, :, :],
-                    in_=pooled[s][:, o, :].rearrange("p (q r) -> p r q", r=2),
-                    func=(ACT.Tanh if o == 0 else ACT.Identity),
-                    bias=bias_col[:, o : o + 1],
-                )
-            pooled_act[s] = acted
+        def activate_phi(s):
+            acted = work.tile([P, 2, P], F32, name="phi_acted")
+            nc.scalar.activation(
+                out=acted[:],
+                in_=pooled[s][:, 0, :].rearrange("p (q r) -> p r q", r=2),
+                func=ACT.Tanh,
+                bias=bias_col[:, 0:1],
+            )
+            phi_act[s] = acted
 
         def store_pooled(s):
             bt = s // SLABS_PER_BATCH
@@ -159,21 +158,23 @@ def tile_selfattention3d_pb_t_kernel(
             phi_t = psum_tr.tile([P, 2, P], F32, tag="tr")
             g_t = psum_tr.tile([P, 2, 2, P], F32, tag="tr")
             for r in range(2):
-                nc.tensor.transpose(phi_t[:, r, :], pooled_act[s][:, 0, r, :], ident_f32[:])
+                nc.tensor.transpose(phi_t[:, r, :], phi_act[s][:, r, :], ident_f32[:])
                 for h in range(2):
                     nc.tensor.transpose(
-                        g_t[:, r, h, :], pooled_act[s][:, 1 + h, r, :], ident_f32[:]
+                        g_t[:, r, h, :], pooled[s][:, 1 + h, r * P : (r + 1) * P], ident_f32[:]
                     )
             phi_out = work.tile([P, 2, P], F32)
             nc.scalar.copy(out=phi_out[:], in_=phi_t[:])
             g_out = work.tile([P, 2, 2 * P], F32)
-            nc.scalar.copy(out=g_out[:], in_=g_t[:].rearrange("p r h c -> p r (h c)"))
+            nc.vector.tensor_add(
+                out=g_out[:], in0=g_t[:].rearrange("p r h c -> p r (h c)"), in1=g_bias[:]
+            )
             nc.sync.dma_start(
                 out=out_1[bt, m0 : m0 + POOLED, :].rearrange("(q r) c -> q r c", r=2),
                 in_=phi_out[:],
             )
             nc.sync.dma_start(
-                out=out_2[bt, m0 : m0 + POOLED, :].rearrange("(q r) c -> q r c", r=2),
+                out=out_2[bt, m0 : m0 + POOLED, :].rearrange("(r q) c -> q r c", r=2),
                 in_=g_out[:],
             )
 
@@ -189,7 +190,14 @@ def tile_selfattention3d_pb_t_kernel(
         bias_rows = consts.tile([P, P], BF16)
         nc.vector.memset(bias_rows[:], 0.0)
         nc.scalar.dma_start(out=bias_rows[0:1, :], in_=b_phi.rearrange("(h c) -> h c", h=1))
-        nc.scalar.dma_start(out=bias_rows[1:3, :], in_=b_g.rearrange("(h c) -> h c", h=2))
+        g_bias_row = consts.tile([P, 2, 2 * P], BF16)
+        nc.vector.memset(g_bias_row[:], 0.0)
+        for r in range(2):
+            nc.scalar.dma_start(
+                out=g_bias_row[0:1, r, :], in_=b_g.rearrange("(h c) -> h c", h=1)
+            )
+        ones = consts.tile([P, P], BF16)
+        nc.vector.memset(ones[:], 1.0)
         nc.scalar.dma_start(
             out=bias_rows[THETA : THETA + 1, :], in_=b_theta.rearrange("(h c) -> h c", h=1)
         )
@@ -229,6 +237,10 @@ def tile_selfattention3d_pb_t_kernel(
         nc.tensor.transpose(bias_t[:], bias_rows[:], ident_bf[:])
         bias_col = consts.tile([P, OUT_TILES], F32)
         nc.vector.tensor_copy(out=bias_col[:], in_=bias_t[:, 0:OUT_TILES])
+        g_bias_t = psum_tr.tile([P, 2, 2 * P], F32, tag="tr")
+        nc.tensor.matmul(g_bias_t[:], lhsT=ones[:], rhs=g_bias_row[:], start=True, stop=True)
+        g_bias = consts.tile([P, 2, 2 * P], F32)
+        nc.scalar.copy(out=g_bias[:], in_=g_bias_t[:])
         for g in range(PASSES):
             nc.vector.quantize_mx(
                 out=w_codes[:, g, :].bitcast(FP8X4),
@@ -253,4 +265,4 @@ def tile_selfattention3d_pb_t_kernel(
                 if h % 2 == 0:
                     store_pooled((h - 1) // 2)
             if h % 2 == 1:
-                activate_pooled(h // 2)
+                activate_phi(h // 2)

@@ -17,19 +17,21 @@ BATCH = 2
 CH = 1024
 PASSES = CH // K_PASS
 LOCS = 16 * 16 * 16
-SLAB = 1024
 CHUNK = 512
+SLAB = 2 * CHUNK
 SLABS_PER_BATCH = LOCS // SLAB
-X_TILES = BATCH * SLABS_PER_BATCH * PASSES
 CHUNKS = BATCH * LOCS // CHUNK
+X_TILES = [(g, h, 1) for h in range(2) for g in range(PASSES)] + [
+    (g, h, 2) for h in range(2, CHUNKS, 2) for g in range(PASSES)
+]
+HEAD_TILES = 4
 OUT_TILES = 4
 POOLED_TILES = 3
 THETA = 3
 POOLED = SLAB // 4
-V_COLS = 160
-G_COLS = 384
-
-LOADS_AHEAD = 6
+V_COLS, G_COLS = 192, 288
+V_HEAD, G_HEAD = 256, 96
+LOADS_AHEAD = 8
 
 FLOPS = 2 * BATCH * LOCS * CH * OUT_TILES * P
 
@@ -42,99 +44,124 @@ def tile_selfattention3d_pb_t_kernel(
 
     with ExitStack() as ctx:
         consts = ctx.enter_context(tc.tile_pool(name="consts", bufs=1))
-        raw_pool = ctx.enter_context(tc.tile_pool(name="raw", bufs=6))
+        raw_pool = ctx.enter_context(tc.tile_pool(name="raw", bufs=LOADS_AHEAD))
         grouped_pool = ctx.enter_context(tc.tile_pool(name="grouped", bufs=3))
         mx_pool = ctx.enter_context(tc.tile_pool(name="mx", bufs=6))
         work = ctx.enter_context(tc.tile_pool(name="work", bufs=3))
-        psum_acc = ctx.enter_context(tc.psum_pool(name="psum_acc", bufs=5))
+        psum_pooled = ctx.enter_context(tc.psum_pool(name="psum_pooled", bufs=4))
+        psum_theta = ctx.enter_context(tc.psum_pool(name="psum_theta", bufs=1))
         psum_tr = ctx.enter_context(tc.psum_pool(name="psum_tr", bufs=3))
 
         raw = {}
         grouped = {}
-        x_codes = {}
-        x_scales = {}
+        x_quantised = {}
+        acc = {}
         theta_act = {}
         pooled = {}
         phi_act = {}
 
         def load(j):
-            s, g = j // PASSES, j % PASSES
-            bt, n0 = s // SLABS_PER_BATCH, (s % SLABS_PER_BATCH) * SLAB
-            rows = raw_pool.tile([P, PACK, SLAB], BF16)
-            nc.sync.dma_start(out=rows[:], in_=x_view[bt, g, :, :, n0 : n0 + SLAB])
+            if j >= len(X_TILES):
+                return
+            g, h, chunks = X_TILES[j]
+            bt, n0 = divmod(h * CHUNK, LOCS)
+            width = chunks * CHUNK
+            rows = raw_pool.tile([P, PACK, width], BF16)
+            nc.sync.dma_start(out=rows[:], in_=x_view[bt, g, :, :, n0 : n0 + width])
             raw[j] = rows
 
-        def regroup(j):
-            quads = grouped_pool.tile([P, SLAB, PACK], BF16, align_bytes=64)
-            dst = quads[:].rearrange("p (c i) t -> p c t i", i=4)
-            src = raw[j][:].rearrange("p t (c i) -> p c t i", i=4)
-            v_end = V_COLS // 4
-            g_end = (V_COLS + G_COLS) // 4
-            nc.vector.tensor_copy(out=dst[:, :v_end], in_=src[:, :v_end])
+        def shares(j):
+            return (V_HEAD, V_HEAD + G_HEAD) if j < HEAD_TILES else (V_COLS, V_COLS + G_COLS)
+
+        def regroup_gpsimd(j):
+            if j >= len(X_TILES):
+                return
+            v_end, g_end = shares(j)
+            quads = grouped_pool.tile([P, X_TILES[j][2] * CHUNK, PACK], BF16, align_bytes=64)
             nc.gpsimd.tensor_scalar(
-                out=quads[:, V_COLS : V_COLS + G_COLS, :],
-                in0=raw[j][:, :, V_COLS : V_COLS + G_COLS].rearrange("p t n -> p n t"),
+                out=quads[:, v_end:g_end, :],
+                in0=raw[j][:, :, v_end:g_end].rearrange("p t n -> p n t"),
                 scalar1=1.0,
                 scalar2=0.0,
                 op0=mybir.AluOpType.mult,
                 op1=mybir.AluOpType.add,
             )
-            nc.scalar.copy(out=dst[:, g_end:], in_=src[:, g_end:])
             grouped[j] = quads
 
+        def regroup(j):
+            if j >= len(X_TILES):
+                return
+            v_end, g_end = shares(j)
+            dst = grouped[j][:].rearrange("p (c i) t -> p c t i", i=4)
+            src = raw[j][:].rearrange("p t (c i) -> p c t i", i=4)
+            nc.vector.tensor_copy(out=dst[:, : v_end // 4], in_=src[:, : v_end // 4])
+            nc.scalar.copy(out=dst[:, g_end // 4 :], in_=src[:, g_end // 4 :])
+
         def quantise(j):
-            codes = mx_pool.tile([P, SLAB], U32, align_bytes=64)
-            scales = mx_pool.tile([P, SLAB], U8, align_bytes=64)
+            if j >= len(X_TILES):
+                return
+            g, h, chunks = X_TILES[j]
+            width = chunks * CHUNK
+            codes = mx_pool.tile([P, width], U32, align_bytes=64)
+            scales = mx_pool.tile([P, width], U8, align_bytes=64)
             nc.vector.quantize_mx(
                 out=codes[:].bitcast(FP8X4),
                 scales=scales[:],
                 in_=grouped[j][:].rearrange("p n t -> p (n t)"),
             )
-            x_codes[j] = codes
-            x_scales[j] = scales
+            for c in range(chunks):
+                cols = slice(c * CHUNK, (c + 1) * CHUNK)
+                x_quantised[(g, h + c)] = (codes[:, cols], scales[:, cols])
 
-        def convolve(s, u):
-            cols = slice(u * CHUNK, (u + 1) * CHUNK)
+        def convolve(h, o, pool):
+            outs = slice(o * P, (o + 1) * P)
+            sums = pool.tile([P, CHUNK], F32)
+            for g in range(PASSES):
+                codes, scales = x_quantised[(g, h)]
+                nc.tensor.matmul_mx(
+                    out=sums[:],
+                    lhsT=w_codes[:, g, outs].bitcast(FP8X4),
+                    lhsT_scale=w_scales[:, g, outs],
+                    rhs=codes.bitcast(FP8X4),
+                    rhs_scale=scales,
+                    start=(g == 0),
+                    stop=(g == PASSES - 1),
+                )
+            acc[(h, o)] = sums
+
+        def convolve_pooled(h):
+            if h < CHUNKS:
+                for o in range(POOLED_TILES):
+                    convolve(h, o, psum_pooled)
+
+        def max_pool(h):
+            s, u = divmod(h, 2)
             if u == 0:
                 pooled[s] = work.tile([P, POOLED_TILES, POOLED], F32, name="pooled_max")
-            for o in range(OUT_TILES):
-                outs = slice(o * P, (o + 1) * P)
-                acc = psum_acc.tile([P, CHUNK], F32)
-                for g in range(PASSES):
-                    nc.tensor.matmul_mx(
-                        out=acc[:],
-                        lhsT=w_codes[:, g, outs].bitcast(FP8X4),
-                        lhsT_scale=w_scales[:, g, outs],
-                        rhs=x_codes[PASSES * s + g][:, cols].bitcast(FP8X4),
-                        rhs_scale=x_scales[PASSES * s + g][:, cols],
-                        start=(g == 0),
-                        stop=(g == PASSES - 1),
-                    )
-                if o < POOLED_TILES:
-                    nc.vector.tensor_reduce(
-                        out=pooled[s][:, o, u * P : (u + 1) * P].rearrange(
-                            "p (r j) -> p r j", j=8
-                        ),
-                        in_=acc[:].rearrange("p (r a j b) -> p r j a b", a=2, j=8, b=2),
-                        axis=mybir.AxisListType.XY,
-                        op=mybir.AluOpType.max,
-                    )
-                else:
-                    th = work.tile([P, 4, P], F32, name="th")
-                    nc.scalar.activation(
-                        out=th[:],
-                        in_=acc[:].rearrange("p (q r) -> p r q", r=4),
-                        func=ACT.Tanh,
-                        bias=bias_col[:, THETA : THETA + 1],
-                    )
-                    theta_act[(s, u)] = th
+            for o in range(POOLED_TILES):
+                nc.vector.tensor_reduce(
+                    out=pooled[s][:, o, u * P : (u + 1) * P].rearrange("p (r j) -> p r j", j=8),
+                    in_=acc[(h, o)][:].rearrange("p (r a j b) -> p r j a b", a=2, j=8, b=2),
+                    axis=mybir.AxisListType.XY,
+                    op=mybir.AluOpType.max,
+                )
 
-        def store_theta(s, u):
-            bt = s // SLABS_PER_BATCH
-            n0 = (s % SLABS_PER_BATCH) * SLAB + u * CHUNK
+        def theta(h):
+            convolve(h, THETA, psum_theta)
+            th = work.tile([P, 4, P], F32, name="th")
+            nc.scalar.activation(
+                out=th[:],
+                in_=acc[(h, THETA)][:].rearrange("p (q r) -> p r q", r=4),
+                func=ACT.Tanh,
+                bias=bias_col[:, THETA : THETA + 1],
+            )
+            theta_act[h] = th
+
+        def store_theta(h):
+            bt, n0 = divmod(h * CHUNK, LOCS)
             th_t = psum_tr.tile([P, 4, P], F32, tag="tr")
             for r in range(4):
-                nc.tensor.transpose(th_t[:, r, :], theta_act[(s, u)][:, r, :], ident_f32[:])
+                nc.tensor.transpose(th_t[:, r, :], theta_act[h][:, r, :], ident_f32[:])
             th_out = work.tile([P, 4, P], F32)
             nc.scalar.copy(out=th_out[:], in_=th_t[:])
             nc.sync.dma_start(
@@ -152,70 +179,71 @@ def tile_selfattention3d_pb_t_kernel(
             )
             phi_act[s] = acted
 
-        def store_pooled(s):
-            bt = s // SLABS_PER_BATCH
-            m0 = (s % SLABS_PER_BATCH) * POOLED
+        def transpose_pooled(s):
             phi_t = psum_tr.tile([P, 2, P], F32, tag="tr")
             g_t = psum_tr.tile([P, 2, 2, P], F32, tag="tr")
             for r in range(2):
-                nc.tensor.transpose(phi_t[:, r, :], phi_act[s][:, r, :], ident_f32[:])
                 for h in range(2):
                     nc.tensor.transpose(
                         g_t[:, r, h, :], pooled[s][:, 1 + h, r * P : (r + 1) * P], ident_f32[:]
                     )
-            phi_out = work.tile([P, 2, P], F32)
-            nc.scalar.copy(out=phi_out[:], in_=phi_t[:])
+            for r in range(2):
+                nc.tensor.transpose(phi_t[:, r, :], phi_act[s][:, r, :], ident_f32[:])
+            return phi_t, g_t
+
+        def store_pooled(s, phi_t, g_t):
+            bt = s // SLABS_PER_BATCH
+            m0 = (s % SLABS_PER_BATCH) * POOLED
             g_out = work.tile([P, 2, 2 * P], F32)
             nc.vector.tensor_add(
                 out=g_out[:], in0=g_t[:].rearrange("p r h c -> p r (h c)"), in1=g_bias[:]
             )
             nc.sync.dma_start(
-                out=out_1[bt, m0 : m0 + POOLED, :].rearrange("(q r) c -> q r c", r=2),
-                in_=phi_out[:],
-            )
-            nc.sync.dma_start(
                 out=out_2[bt, m0 : m0 + POOLED, :].rearrange("(r q) c -> q r c", r=2),
                 in_=g_out[:],
             )
+            phi_out = work.tile([P, 2, P], F32)
+            nc.scalar.copy(out=phi_out[:], in_=phi_t[:])
+            nc.sync.dma_start(
+                out=out_1[bt, m0 : m0 + POOLED, :].rearrange("(q r) c -> q r c", r=2),
+                in_=phi_out[:],
+            )
 
-        load(0)
-        load(1)
+        ctx.enter_context(tc.manual_schedule())
+
         w_rows = consts.tile([P, OUT_TILES, CH], BF16)
         nc.sync.dma_start(out=w_rows[:, 0, :], in_=w_phi)
         nc.sync.dma_start(out=w_rows[:, 1:3, :], in_=w_g.rearrange("(h o) k -> o h k", h=2))
         nc.sync.dma_start(out=w_rows[:, THETA, :], in_=w_theta)
-        for j in range(2, LOADS_AHEAD):
+        for j in range(LOADS_AHEAD):
             load(j)
 
+        ident_f32 = consts.tile([P, P], F32)
+        make_identity(nc, ident_f32[:])
         bias_rows = consts.tile([P, P], BF16)
         nc.vector.memset(bias_rows[:], 0.0)
-        nc.scalar.dma_start(out=bias_rows[0:1, :], in_=b_phi.rearrange("(h c) -> h c", h=1))
         g_bias_row = consts.tile([P, 2, 2 * P], BF16)
         nc.vector.memset(g_bias_row[:], 0.0)
+        ones = consts.tile([P, P], BF16)
+        nc.vector.memset(ones[:], 1.0)
+        nc.scalar.dma_start(out=bias_rows[0:1, :], in_=b_phi.rearrange("(h c) -> h c", h=1))
+        nc.scalar.dma_start(
+            out=bias_rows[THETA : THETA + 1, :], in_=b_theta.rearrange("(h c) -> h c", h=1)
+        )
         for r in range(2):
             nc.scalar.dma_start(
                 out=g_bias_row[0:1, r, :], in_=b_g.rearrange("(h c) -> h c", h=1)
             )
-        ones = consts.tile([P, P], BF16)
-        nc.vector.memset(ones[:], 1.0)
-        nc.scalar.dma_start(
-            out=bias_rows[THETA : THETA + 1, :], in_=b_theta.rearrange("(h c) -> h c", h=1)
-        )
         ident_bf = consts.tile([P, P], BF16)
         make_identity(nc, ident_bf[:])
-        ident_f32 = consts.tile([P, P], F32)
-        make_identity(nc, ident_f32[:])
-
-        regroup(0)
-        regroup(1)
 
         w_grouped = consts.tile([P, PASSES, OUT_TILES * P, PACK], BF16, align_bytes=64)
         w_codes = consts.tile([P, PASSES, OUT_TILES * P], U32, align_bytes=64)
         w_scales = consts.tile([P, PASSES, OUT_TILES * P], U8, align_bytes=64)
         w_words = w_rows[:].bitcast(F32)
         w_grouped_words = w_grouped[:].bitcast(F32)
-        for g in range(PASSES):
-            for h in range(2):
+        for h in range(2):
+            for g in range(PASSES):
                 w_t = psum_tr.tile([P, 2, 2, P], F32, tag="tr")
                 for o in range(2):
                     for u in range(2):
@@ -229,40 +257,58 @@ def tile_selfattention3d_pb_t_kernel(
                     "p (o r) u -> p o r u", o=2
                 )
                 src = w_t[:].rearrange("p o u r -> p o r u")
-                if h == 0:
+                if g == 0:
                     nc.vector.tensor_copy(out=dst, in_=src)
                 else:
                     nc.scalar.copy(out=dst, in_=src)
         bias_t = psum_tr.tile([P, P], BF16, tag="tr")
         nc.tensor.transpose(bias_t[:], bias_rows[:], ident_bf[:])
-        bias_col = consts.tile([P, OUT_TILES], F32)
-        nc.vector.tensor_copy(out=bias_col[:], in_=bias_t[:, 0:OUT_TILES])
         g_bias_t = psum_tr.tile([P, 2, 2 * P], F32, tag="tr")
         nc.tensor.matmul(g_bias_t[:], lhsT=ones[:], rhs=g_bias_row[:], start=True, stop=True)
-        g_bias = consts.tile([P, 2, 2 * P], F32)
-        nc.scalar.copy(out=g_bias[:], in_=g_bias_t[:])
+
+        for j in range(3):
+            regroup_gpsimd(j)
+        regroup(0)
         for g in range(PASSES):
             nc.vector.quantize_mx(
                 out=w_codes[:, g, :].bitcast(FP8X4),
                 scales=w_scales[:, g, :],
                 in_=w_grouped[:, g, :, :].rearrange("p r t -> p (r t)"),
             )
+        regroup(1)
         quantise(0)
         regroup(2)
         quantise(1)
+        regroup_gpsimd(3)
+        regroup_gpsimd(4)
+        bias_col = consts.tile([P, OUT_TILES], F32)
+        nc.vector.tensor_copy(out=bias_col[:], in_=bias_t[:, 0:OUT_TILES])
+        g_bias = consts.tile([P, 2, 2 * P], F32)
+        nc.scalar.copy(out=g_bias[:], in_=g_bias_t[:])
+        convolve_pooled(0)
+        quantise(2)
+        regroup(3)
+        regroup_gpsimd(5)
+        regroup(4)
+        quantise(3)
+        regroup_gpsimd(6)
 
         for h in range(CHUNKS + 1):
-            if h + LOADS_AHEAD < X_TILES:
-                load(h + LOADS_AHEAD)
-            if h + 3 < X_TILES:
-                regroup(h + 3)
-            if h + 2 < X_TILES:
-                quantise(h + 2)
+            load(h + LOADS_AHEAD)
+            regroup(h + 5)
+            quantise(h + 4)
+            regroup_gpsimd(h + 7)
             if h < CHUNKS:
-                convolve(h // 2, h % 2)
+                theta(h)
             if h > 0:
-                store_theta((h - 1) // 2, (h - 1) % 2)
-                if h % 2 == 0:
-                    store_pooled((h - 1) // 2)
+                store_theta(h - 1)
+            slab_done = h > 0 and h % 2 == 0
+            if slab_done:
+                transposed = transpose_pooled(h // 2 - 1)
+            if h < CHUNKS:
+                max_pool(h)
+            if slab_done:
+                store_pooled(h // 2 - 1, *transposed)
             if h % 2 == 1:
                 activate_phi(h // 2)
+            convolve_pooled(h + 1)

@@ -21,17 +21,21 @@ CHUNK = 512
 SLAB = 2 * CHUNK
 SLABS_PER_BATCH = LOCS // SLAB
 CHUNKS = BATCH * LOCS // CHUNK
-X_TILES = [(g, h, 1) for h in range(2) for g in range(PASSES)] + [
-    (g, h, 2) for h in range(2, CHUNKS, 2) for g in range(PASSES)
-]
+LAST = CHUNKS - 1
+X_TILES = (
+    [(g, h, 1) for h in range(2) for g in range(PASSES)]
+    + [(g, h, 2) for h in range(2, CHUNKS - 2, 2) for g in range(PASSES)]
+    + [(g, h, 1) for h in (LAST - 1, LAST) for g in range(PASSES)]
+)
 HEAD_TILES = 4
+TAIL_TILES = 4
 OUT_TILES = 4
 POOLED_TILES = 3
 THETA = 3
 POOLED = SLAB // 4
-V_COLS, G_COLS = 192, 288
+V_COLS, G_COLS = 160, 384
 V_HEAD, G_HEAD = 256, 96
-LOADS_AHEAD = 8
+LOADS_AHEAD = 10
 
 FLOPS = 2 * BATCH * LOCS * CH * OUT_TILES * P
 
@@ -45,7 +49,7 @@ def tile_selfattention3d_pb_t_kernel(
     with ExitStack() as ctx:
         consts = ctx.enter_context(tc.tile_pool(name="consts", bufs=1))
         raw_pool = ctx.enter_context(tc.tile_pool(name="raw", bufs=LOADS_AHEAD))
-        grouped_pool = ctx.enter_context(tc.tile_pool(name="grouped", bufs=3))
+        grouped_pool = ctx.enter_context(tc.tile_pool(name="grouped", bufs=4))
         mx_pool = ctx.enter_context(tc.tile_pool(name="mx", bufs=6))
         work = ctx.enter_context(tc.tile_pool(name="work", bufs=3))
         psum_pooled = ctx.enter_context(tc.psum_pool(name="psum_pooled", bufs=4))
@@ -71,7 +75,10 @@ def tile_selfattention3d_pb_t_kernel(
             raw[j] = rows
 
         def shares(j):
-            return (V_HEAD, V_HEAD + G_HEAD) if j < HEAD_TILES else (V_COLS, V_COLS + G_COLS)
+            if j < HEAD_TILES:
+                return V_HEAD, V_HEAD + G_HEAD
+            width = X_TILES[j][2] * CHUNK
+            return V_COLS * width // SLAB, (V_COLS + G_COLS) * width // SLAB
 
         def regroup_gpsimd(j):
             if j >= len(X_TILES):
@@ -146,8 +153,7 @@ def tile_selfattention3d_pb_t_kernel(
                     op=mybir.AluOpType.max,
                 )
 
-        def theta(h):
-            convolve(h, THETA, psum_theta)
+        def activate_theta(h):
             th = work.tile([P, 4, P], F32, name="th")
             nc.scalar.activation(
                 out=th[:],
@@ -169,44 +175,48 @@ def tile_selfattention3d_pb_t_kernel(
                 in_=th_out[:],
             )
 
-        def activate_phi(s):
-            acted = work.tile([P, 2, P], F32, name="phi_acted")
+        def activate_phi(s, u0, runs):
+            acted = work.tile([P, runs, P], F32, name="phi_acted")
             nc.scalar.activation(
                 out=acted[:],
-                in_=pooled[s][:, 0, :].rearrange("p (q r) -> p r q", r=2),
+                in_=pooled[s][:, 0, u0 * P : (u0 + runs) * P].rearrange(
+                    "p (q r) -> p r q", r=runs
+                ),
                 func=ACT.Tanh,
                 bias=bias_col[:, 0:1],
             )
             phi_act[s] = acted
 
-        def transpose_pooled(s):
-            phi_t = psum_tr.tile([P, 2, P], F32, tag="tr")
-            g_t = psum_tr.tile([P, 2, 2, P], F32, tag="tr")
-            for r in range(2):
+        def transpose_pooled(s, u0, runs):
+            g_t = psum_tr.tile([P, runs, 2, P], F32, tag="tr")
+            for r in range(runs):
+                n0 = (u0 + r) * P
                 for h in range(2):
                     nc.tensor.transpose(
-                        g_t[:, r, h, :], pooled[s][:, 1 + h, r * P : (r + 1) * P], ident_f32[:]
+                        g_t[:, r, h, :], pooled[s][:, 1 + h, n0 : n0 + P], ident_f32[:]
                     )
-            for r in range(2):
+            phi_t = psum_tr.tile([P, runs, P], F32, tag="tr")
+            for r in range(runs):
                 nc.tensor.transpose(phi_t[:, r, :], phi_act[s][:, r, :], ident_f32[:])
             return phi_t, g_t
 
-        def store_pooled(s, phi_t, g_t):
+        def store_pooled(s, u0, runs, phi_t, g_t):
             bt = s // SLABS_PER_BATCH
-            m0 = (s % SLABS_PER_BATCH) * POOLED
-            g_out = work.tile([P, 2, 2 * P], F32)
+            m0 = (s % SLABS_PER_BATCH) * POOLED + u0 * P
+            m1 = m0 + runs * P
+            g_out = work.tile([P, runs, 2 * P], F32)
             nc.vector.tensor_add(
-                out=g_out[:], in0=g_t[:].rearrange("p r h c -> p r (h c)"), in1=g_bias[:]
+                out=g_out[:],
+                in0=g_t[:].rearrange("p r h c -> p r (h c)"),
+                in1=g_bias[:, :runs, :],
             )
             nc.sync.dma_start(
-                out=out_2[bt, m0 : m0 + POOLED, :].rearrange("(r q) c -> q r c", r=2),
-                in_=g_out[:],
+                out=out_2[bt, m0:m1, :].rearrange("(r q) c -> q r c", r=runs), in_=g_out[:]
             )
-            phi_out = work.tile([P, 2, P], F32)
+            phi_out = work.tile([P, runs, P], F32)
             nc.scalar.copy(out=phi_out[:], in_=phi_t[:])
             nc.sync.dma_start(
-                out=out_1[bt, m0 : m0 + POOLED, :].rearrange("(q r) c -> q r c", r=2),
-                in_=phi_out[:],
+                out=out_1[bt, m0:m1, :].rearrange("(q r) c -> q r c", r=runs), in_=phi_out[:]
             )
 
         ctx.enter_context(tc.manual_schedule())
@@ -292,23 +302,45 @@ def tile_selfattention3d_pb_t_kernel(
         regroup(4)
         quantise(3)
         regroup_gpsimd(6)
+        regroup_gpsimd(7)
 
-        for h in range(CHUNKS + 1):
-            load(h + LOADS_AHEAD)
-            regroup(h + 5)
-            quantise(h + 4)
-            regroup_gpsimd(h + 7)
-            if h < CHUNKS:
-                theta(h)
+        tail = len(X_TILES) - TAIL_TILES
+        to_quantise = [[j] for j in range(HEAD_TILES, tail)]
+        to_quantise += [[tail, tail + 1], [tail + 2, tail + 3], [], []]
+        to_load, to_gather = HEAD_TILES + 6, HEAD_TILES + 4
+        for h in range(CHUNKS):
+            for j in to_quantise[h]:
+                load(to_load)
+                to_load += 1
+            for j in to_quantise[h + 1] if h < LAST else []:
+                regroup(j)
+            for j in to_quantise[h]:
+                quantise(j)
+                regroup_gpsimd(to_gather)
+                to_gather += 1
+            if h < LAST:
+                convolve(h, THETA, psum_theta)
+                activate_theta(h)
             if h > 0:
                 store_theta(h - 1)
-            slab_done = h > 0 and h % 2 == 0
-            if slab_done:
-                transposed = transpose_pooled(h // 2 - 1)
-            if h < CHUNKS:
-                max_pool(h)
-            if slab_done:
-                store_pooled(h // 2 - 1, *transposed)
-            if h % 2 == 1:
-                activate_phi(h // 2)
+            done = None
+            if h == LAST:
+                done = h // 2, 0, 1
+            elif h > 0 and h % 2 == 0:
+                done = h // 2 - 1, 0, 2
+            if done:
+                transposed = transpose_pooled(*done)
+            max_pool(h)
+            if done:
+                store_pooled(*done, *transposed)
+            if h == LAST - 1:
+                activate_phi(h // 2, 0, 1)
+                convolve(LAST, THETA, psum_theta)
+                activate_theta(LAST)
+            elif h == LAST:
+                activate_phi(h // 2, 1, 1)
+            elif h % 2 == 1:
+                activate_phi(h // 2, 0, 2)
             convolve_pooled(h + 1)
+        store_theta(LAST)
+        store_pooled(LAST // 2, 1, 1, *transpose_pooled(LAST // 2, 1, 1))

@@ -33,7 +33,7 @@ OUT_TILES = 4
 POOLED_TILES = 3
 THETA = 3
 POOLED = SLAB // 4
-V_COLS, G_COLS = 160, 384
+V_COLS, G_COLS = 256, 256
 V_HEAD, G_HEAD = 256, 96
 LOADS_AHEAD = 10
 
@@ -306,41 +306,57 @@ def tile_selfattention3d_pb_t_kernel(
 
         tail = len(X_TILES) - TAIL_TILES
         to_quantise = [[j] for j in range(HEAD_TILES, tail)]
-        to_quantise += [[tail, tail + 1], [tail + 2, tail + 3], [], []]
+        to_quantise += [[tail, tail + 1], [tail + 2, tail + 3]]
         to_load, to_gather = HEAD_TILES + 6, HEAD_TILES + 4
-        for h in range(CHUNKS):
+        for h in range(LAST - 2):
             for j in to_quantise[h]:
                 load(to_load)
                 to_load += 1
-            for j in to_quantise[h + 1] if h < LAST else []:
-                regroup(j)
-            for j in to_quantise[h]:
                 quantise(j)
                 regroup_gpsimd(to_gather)
                 to_gather += 1
-            if h < LAST:
-                convolve(h, THETA, psum_theta)
-                activate_theta(h)
+            for j in to_quantise[h + 1]:
+                regroup(j)
+            convolve(h, THETA, psum_theta)
+            activate_theta(h)
             if h > 0:
                 store_theta(h - 1)
-            done = None
-            if h == LAST:
-                done = h // 2, 0, 1
-            elif h > 0 and h % 2 == 0:
-                done = h // 2 - 1, 0, 2
-            if done:
-                transposed = transpose_pooled(*done)
+            slab_done = h > 0 and h % 2 == 0
+            if slab_done:
+                transposed = transpose_pooled(h // 2 - 1, 0, 2)
             max_pool(h)
-            if done:
-                store_pooled(*done, *transposed)
-            if h == LAST - 1:
-                activate_phi(h // 2, 0, 1)
-                convolve(LAST, THETA, psum_theta)
-                activate_theta(LAST)
-            elif h == LAST:
-                activate_phi(h // 2, 1, 1)
-            elif h % 2 == 1:
+            if slab_done:
+                store_pooled(h // 2 - 1, 0, 2, *transposed)
+            if h % 2 == 1:
                 activate_phi(h // 2, 0, 2)
             convolve_pooled(h + 1)
+
+        s = LAST // 2
+        convolve(LAST - 2, THETA, psum_theta)
+        activate_theta(LAST - 2)
+        store_theta(LAST - 3)
+        max_pool(LAST - 2)
+        activate_phi(s - 1, 0, 2)
+        for j in to_quantise[LAST - 2]:
+            quantise(j)
+        convolve_pooled(LAST - 1)
+        convolve(LAST - 1, THETA, psum_theta)
+        activate_theta(LAST - 1)
+
+        store_theta(LAST - 2)
+        transposed = transpose_pooled(s - 1, 0, 2)
+        max_pool(LAST - 1)
+        store_pooled(s - 1, 0, 2, *transposed)
+        activate_phi(s, 0, 1)
+        convolve_pooled(LAST)
+        convolve(LAST, THETA, psum_theta)
+        activate_theta(LAST)
+
+        store_theta(LAST - 1)
+        transposed = transpose_pooled(s, 0, 1)
+        max_pool(LAST)
+        store_pooled(s, 0, 1, *transposed)
+        activate_phi(s, 1, 1)
+        transposed = transpose_pooled(s, 1, 1)
         store_theta(LAST)
-        store_pooled(LAST // 2, 1, 1, *transpose_pooled(LAST // 2, 1, 1))
+        store_pooled(s, 1, 1, *transposed)

@@ -33,8 +33,10 @@ OUT_TILES = 4
 POOLED_TILES = 3
 THETA = 3
 POOLED = SLAB // 4
-V_COLS, G_COLS = 256, 256
-V_HEAD, G_HEAD = 256, 96
+V_COLS, G_COLS = 160, 352
+V_SMALL = 256
+V_ALONE, ALONE = 448, 8
+GROUPED_BUFS = 3
 LOADS_AHEAD = 10
 
 FLOPS = 2 * BATCH * LOCS * CH * OUT_TILES * P
@@ -49,9 +51,11 @@ def tile_selfattention3d_pb_t_kernel(
     with ExitStack() as ctx:
         consts = ctx.enter_context(tc.tile_pool(name="consts", bufs=1))
         raw_pool = ctx.enter_context(tc.tile_pool(name="raw", bufs=LOADS_AHEAD))
-        grouped_pool = ctx.enter_context(tc.tile_pool(name="grouped", bufs=4))
+        grouped_pool = ctx.enter_context(tc.tile_pool(name="grouped", bufs=GROUPED_BUFS))
+        small_pool = ctx.enter_context(tc.tile_pool(name="small", bufs=4))
         mx_pool = ctx.enter_context(tc.tile_pool(name="mx", bufs=6))
         work = ctx.enter_context(tc.tile_pool(name="work", bufs=3))
+        out_pool = ctx.enter_context(tc.tile_pool(name="out", bufs=6))
         psum_pooled = ctx.enter_context(tc.psum_pool(name="psum_pooled", bufs=4))
         psum_theta = ctx.enter_context(tc.psum_pool(name="psum_theta", bufs=1))
         psum_tr = ctx.enter_context(tc.psum_pool(name="psum_tr", bufs=3))
@@ -75,16 +79,20 @@ def tile_selfattention3d_pb_t_kernel(
             raw[j] = rows
 
         def shares(j):
-            if j < HEAD_TILES:
-                return V_HEAD, V_HEAD + G_HEAD
-            width = X_TILES[j][2] * CHUNK
-            return V_COLS * width // SLAB, (V_COLS + G_COLS) * width // SLAB
+            if X_TILES[j][2] == 1:
+                return V_SMALL, V_SMALL
+            if j <= ALONE:
+                return V_ALONE, V_ALONE
+            return V_COLS, V_COLS + G_COLS
 
-        def regroup_gpsimd(j):
-            if j >= len(X_TILES):
-                return
+        def start_regroup(j):
+            chunks = X_TILES[j][2]
+            pool = small_pool if chunks == 1 else grouped_pool
+            quads = pool.tile([P, chunks * CHUNK, PACK], BF16, align_bytes=64)
+            grouped[j] = quads
             v_end, g_end = shares(j)
-            quads = grouped_pool.tile([P, X_TILES[j][2] * CHUNK, PACK], BF16, align_bytes=64)
+            if g_end == v_end:
+                return
             nc.gpsimd.tensor_scalar(
                 out=quads[:, v_end:g_end, :],
                 in0=raw[j][:, :, v_end:g_end].rearrange("p t n -> p n t"),
@@ -93,20 +101,27 @@ def tile_selfattention3d_pb_t_kernel(
                 op0=mybir.AluOpType.mult,
                 op1=mybir.AluOpType.add,
             )
-            grouped[j] = quads
 
-        def regroup(j):
-            if j >= len(X_TILES):
-                return
-            v_end, g_end = shares(j)
+        def in_runs_of_four(j):
             dst = grouped[j][:].rearrange("p (c i) t -> p c t i", i=4)
             src = raw[j][:].rearrange("p t (c i) -> p c t i", i=4)
-            nc.vector.tensor_copy(out=dst[:, : v_end // 4], in_=src[:, : v_end // 4])
-            nc.scalar.copy(out=dst[:, g_end // 4 :], in_=src[:, g_end // 4 :])
+            return dst, src
+
+        def regroup_vector(j):
+            end = shares(j)[0] // 4
+            dst, src = in_runs_of_four(j)
+            nc.vector.tensor_copy(out=dst[:, :end], in_=src[:, :end])
+
+        def regroup_scalar(j):
+            start = shares(j)[1] // 4
+            dst, src = in_runs_of_four(j)
+            nc.scalar.copy(out=dst[:, start:], in_=src[:, start:])
+
+        def regroup(j):
+            regroup_vector(j)
+            regroup_scalar(j)
 
         def quantise(j):
-            if j >= len(X_TILES):
-                return
             g, h, chunks = X_TILES[j]
             width = chunks * CHUNK
             codes = mx_pool.tile([P, width], U32, align_bytes=64)
@@ -136,11 +151,6 @@ def tile_selfattention3d_pb_t_kernel(
                 )
             acc[(h, o)] = sums
 
-        def convolve_pooled(h):
-            if h < CHUNKS:
-                for o in range(POOLED_TILES):
-                    convolve(h, o, psum_pooled)
-
         def max_pool(h):
             s, u = divmod(h, 2)
             if u == 0:
@@ -163,13 +173,13 @@ def tile_selfattention3d_pb_t_kernel(
             )
             theta_act[h] = th
 
-        def store_theta(h):
+        def store_theta(h, copy=nc.scalar.copy, pool=psum_tr, tag="tr"):
             bt, n0 = divmod(h * CHUNK, LOCS)
-            th_t = psum_tr.tile([P, 4, P], F32, tag="tr")
+            th_t = pool.tile([P, 4, P], F32, tag=tag)
             for r in range(4):
                 nc.tensor.transpose(th_t[:, r, :], theta_act[h][:, r, :], ident_f32[:])
-            th_out = work.tile([P, 4, P], F32)
-            nc.scalar.copy(out=th_out[:], in_=th_t[:])
+            th_out = out_pool.tile([P, 4, P], F32)
+            copy(out=th_out[:], in_=th_t[:])
             nc.sync.dma_start(
                 out=out_0[bt, n0 : n0 + CHUNK, :].rearrange("(q r) c -> q r c", r=4),
                 in_=th_out[:],
@@ -185,7 +195,7 @@ def tile_selfattention3d_pb_t_kernel(
                 func=ACT.Tanh,
                 bias=bias_col[:, 0:1],
             )
-            phi_act[s] = acted
+            phi_act[(s, u0)] = acted
 
         def transpose_pooled(s, u0, runs):
             g_t = psum_tr.tile([P, runs, 2, P], F32, tag="tr")
@@ -197,36 +207,30 @@ def tile_selfattention3d_pb_t_kernel(
                     )
             phi_t = psum_tr.tile([P, runs, P], F32, tag="tr")
             for r in range(runs):
-                nc.tensor.transpose(phi_t[:, r, :], phi_act[s][:, r, :], ident_f32[:])
+                nc.tensor.transpose(phi_t[:, r, :], phi_act[(s, u0)][:, r, :], ident_f32[:])
             return phi_t, g_t
 
-        def store_pooled(s, u0, runs, phi_t, g_t):
+        def store_pooled(s, u0, runs, phi_t, g_t, gpsimd_adds=False):
             bt = s // SLABS_PER_BATCH
             m0 = (s % SLABS_PER_BATCH) * POOLED + u0 * P
             m1 = m0 + runs * P
-            g_out = work.tile([P, runs, 2 * P], F32)
-            nc.vector.tensor_add(
-                out=g_out[:],
-                in0=g_t[:].rearrange("p r h c -> p r (h c)"),
-                in1=g_bias[:, :runs, :],
-            )
+            g_out = out_pool.tile([P, runs, 2 * P], F32)
+            g_rows = g_t[:].rearrange("p r h c -> p r (h c)")
+            if gpsimd_adds:
+                nc.scalar.copy(out=g_out[:], in_=g_rows)
+                nc.gpsimd.tensor_add(out=g_out[:], in0=g_out[:], in1=g_bias[:, :runs, :])
+            else:
+                nc.vector.tensor_add(out=g_out[:], in0=g_rows, in1=g_bias[:, :runs, :])
             nc.sync.dma_start(
                 out=out_2[bt, m0:m1, :].rearrange("(r q) c -> q r c", r=runs), in_=g_out[:]
             )
-            phi_out = work.tile([P, runs, P], F32)
+            phi_out = out_pool.tile([P, runs, P], F32)
             nc.scalar.copy(out=phi_out[:], in_=phi_t[:])
             nc.sync.dma_start(
                 out=out_1[bt, m0:m1, :].rearrange("(q r) c -> q r c", r=runs), in_=phi_out[:]
             )
 
         ctx.enter_context(tc.manual_schedule())
-
-        w_rows = consts.tile([P, OUT_TILES, CH], BF16)
-        nc.sync.dma_start(out=w_rows[:, 0, :], in_=w_phi)
-        nc.sync.dma_start(out=w_rows[:, 1:3, :], in_=w_g.rearrange("(h o) k -> o h k", h=2))
-        nc.sync.dma_start(out=w_rows[:, THETA, :], in_=w_theta)
-        for j in range(LOADS_AHEAD):
-            load(j)
 
         ident_f32 = consts.tile([P, P], F32)
         make_identity(nc, ident_f32[:])
@@ -244,6 +248,12 @@ def tile_selfattention3d_pb_t_kernel(
             nc.scalar.dma_start(
                 out=g_bias_row[0:1, r, :], in_=b_g.rearrange("(h c) -> h c", h=1)
             )
+        w_rows = consts.tile([P, OUT_TILES, CH], BF16)
+        for o, rows in enumerate((w_phi, w_g[:P, :], w_g[P:, :], w_theta)):
+            nc.sync.dma_start(out=w_rows[:, o, :], in_=rows)
+        for j in range(LOADS_AHEAD):
+            load(j)
+
         ident_bf = consts.tile([P, P], BF16)
         make_identity(nc, ident_bf[:])
 
@@ -252,76 +262,102 @@ def tile_selfattention3d_pb_t_kernel(
         w_scales = consts.tile([P, PASSES, OUT_TILES * P], U8, align_bytes=64)
         w_words = w_rows[:].bitcast(F32)
         w_grouped_words = w_grouped[:].bitcast(F32)
-        for h in range(2):
+        for o in range(OUT_TILES):
+            w_t = psum_tr.tile([P, PASSES, 2, P], F32, tag="tr")
             for g in range(PASSES):
-                w_t = psum_tr.tile([P, 2, 2, P], F32, tag="tr")
-                for o in range(2):
-                    for u in range(2):
-                        w0 = g * (K_PASS // 2)
-                        nc.tensor.transpose(
-                            w_t[:, o, u, :],
-                            w_words[:, 2 * h + o, w0 + u : w0 + K_PASS // 2 : 2],
-                            ident_f32[:],
-                        )
-                dst = w_grouped_words[:, g, 2 * h * P : (2 * h + 2) * P, :].rearrange(
-                    "p (o r) u -> p o r u", o=2
-                )
-                src = w_t[:].rearrange("p o u r -> p o r u")
-                if g == 0:
-                    nc.vector.tensor_copy(out=dst, in_=src)
-                else:
-                    nc.scalar.copy(out=dst, in_=src)
-        bias_t = psum_tr.tile([P, P], BF16, tag="tr")
-        nc.tensor.transpose(bias_t[:], bias_rows[:], ident_bf[:])
-        g_bias_t = psum_tr.tile([P, 2, 2 * P], F32, tag="tr")
-        nc.tensor.matmul(g_bias_t[:], lhsT=ones[:], rhs=g_bias_row[:], start=True, stop=True)
+                for u in range(2):
+                    w0 = g * (K_PASS // 2)
+                    nc.tensor.transpose(
+                        w_t[:, g, u, :],
+                        w_words[:, o, w0 + u : w0 + K_PASS // 2 : 2],
+                        ident_f32[:],
+                    )
+            dst = w_grouped_words[:, :, o * P : (o + 1) * P, :]
+            src = w_t[:].rearrange("p g u r -> p g r u")
+            if o % 2 == 0:
+                nc.vector.tensor_copy(out=dst, in_=src)
+            else:
+                nc.scalar.copy(out=dst, in_=src)
 
-        for j in range(3):
-            regroup_gpsimd(j)
-        regroup(0)
-        for g in range(PASSES):
+        def quantise_weights(g):
             nc.vector.quantize_mx(
                 out=w_codes[:, g, :].bitcast(FP8X4),
                 scales=w_scales[:, g, :],
                 in_=w_grouped[:, g, :, :].rearrange("p r t -> p (r t)"),
             )
+
+        bias_t = psum_tr.tile([P, P], BF16, tag="tr")
+        nc.tensor.transpose(bias_t[:], bias_rows[:], ident_bf[:])
+        for j in range(HEAD_TILES + GROUPED_BUFS):
+            start_regroup(j)
+        regroup(0)
+        quantise_weights(0)
         regroup(1)
+        quantise_weights(1)
         quantise(0)
-        regroup(2)
         quantise(1)
-        regroup_gpsimd(3)
-        regroup_gpsimd(4)
+        regroup(2)
+        regroup(3)
         bias_col = consts.tile([P, OUT_TILES], F32)
         nc.vector.tensor_copy(out=bias_col[:], in_=bias_t[:, 0:OUT_TILES])
+
+        def pooled_matmuls(h):
+            for o in range(POOLED_TILES):
+                convolve(h, o, psum_pooled)
+
+        pooled_matmuls(0)
+        g_bias_t = psum_tr.tile([P, 2, 2 * P], F32, tag="tr")
+        nc.tensor.matmul(g_bias_t[:], lhsT=ones[:], rhs=g_bias_row[:], start=True, stop=True)
+        quantise(2)
+        quantise(3)
+        convolve(0, THETA, psum_theta)
+        regroup_scalar(4)
+        activate_theta(0)
         g_bias = consts.tile([P, 2, 2 * P], F32)
         nc.scalar.copy(out=g_bias[:], in_=g_bias_t[:])
-        convolve_pooled(0)
-        quantise(2)
-        regroup(3)
-        regroup_gpsimd(5)
-        regroup(4)
-        quantise(3)
-        regroup_gpsimd(6)
-        regroup_gpsimd(7)
+        max_pool(0)
+        pooled_matmuls(1)
+        regroup_vector(4)
+        regroup_scalar(5)
+        store_theta(0)
+        convolve(1, THETA, psum_theta)
+        activate_theta(1)
+        regroup_scalar(6)
+        max_pool(1)
+        activate_phi(0, 0, 2)
+        quantise(4)
+        regroup_vector(5)
+        quantise(5)
+        pooled_matmuls(2)
+        regroup_vector(6)
 
         tail = len(X_TILES) - TAIL_TILES
-        to_quantise = [[j] for j in range(HEAD_TILES, tail)]
+        to_quantise = [[], [], *[[j] for j in range(6, tail)]]
         to_quantise += [[tail, tail + 1], [tail + 2, tail + 3]]
-        to_load, to_gather = HEAD_TILES + 6, HEAD_TILES + 4
-        for h in range(LAST - 2):
+        to_load, to_start = LOADS_AHEAD, HEAD_TILES + GROUPED_BUFS
+        for j in range(2):
+            start_regroup(to_start)
+            to_start += 1
+        for j in range(4):
+            load(to_load)
+            to_load += 1
+        for h in range(2, LAST - 2):
             for j in to_quantise[h]:
                 load(to_load)
                 to_load += 1
                 quantise(j)
-                regroup_gpsimd(to_gather)
-                to_gather += 1
+                if to_start < len(X_TILES):
+                    start_regroup(to_start)
+                    to_start += 1
             for j in to_quantise[h + 1]:
+                while to_start <= j:
+                    start_regroup(to_start)
+                    to_start += 1
                 regroup(j)
             convolve(h, THETA, psum_theta)
             activate_theta(h)
-            if h > 0:
-                store_theta(h - 1)
-            slab_done = h > 0 and h % 2 == 0
+            store_theta(h - 1)
+            slab_done = h % 2 == 0
             if slab_done:
                 transposed = transpose_pooled(h // 2 - 1, 0, 2)
             max_pool(h)
@@ -329,7 +365,7 @@ def tile_selfattention3d_pb_t_kernel(
                 store_pooled(h // 2 - 1, 0, 2, *transposed)
             if h % 2 == 1:
                 activate_phi(h // 2, 0, 2)
-            convolve_pooled(h + 1)
+            pooled_matmuls(h + 1)
 
         s = LAST // 2
         convolve(LAST - 2, THETA, psum_theta)
@@ -339,24 +375,25 @@ def tile_selfattention3d_pb_t_kernel(
         activate_phi(s - 1, 0, 2)
         for j in to_quantise[LAST - 2]:
             quantise(j)
-        convolve_pooled(LAST - 1)
+        convolve(LAST - 1, 0, psum_pooled)
+        convolve(LAST - 1, 1, psum_pooled)
         convolve(LAST - 1, THETA, psum_theta)
         activate_theta(LAST - 1)
-
+        convolve(LAST - 1, 2, psum_pooled)
+        max_pool(LAST - 1)
         store_theta(LAST - 2)
         transposed = transpose_pooled(s - 1, 0, 2)
-        max_pool(LAST - 1)
-        store_pooled(s - 1, 0, 2, *transposed)
+        convolve(LAST, 0, psum_pooled)
         activate_phi(s, 0, 1)
-        convolve_pooled(LAST)
         convolve(LAST, THETA, psum_theta)
         activate_theta(LAST)
-
-        store_theta(LAST - 1)
-        transposed = transpose_pooled(s, 0, 1)
+        for o in range(1, POOLED_TILES):
+            convolve(LAST, o, psum_pooled)
+        store_pooled(s - 1, 0, 2, *transposed)
         max_pool(LAST)
-        store_pooled(s, 0, 1, *transposed)
+        store_theta(LAST - 1, nc.vector.tensor_copy, pool=psum_pooled, tag="sums")
         activate_phi(s, 1, 1)
-        transposed = transpose_pooled(s, 1, 1)
-        store_theta(LAST)
-        store_pooled(s, 1, 1, *transposed)
+        transposed = transpose_pooled(s, 0, 1)
+        store_pooled(s, 0, 1, *transposed)
+        store_theta(LAST, pool=psum_pooled, tag="sums")
+        store_pooled(s, 1, 1, *transpose_pooled(s, 1, 1))

@@ -29,14 +29,18 @@ X_TILES = (
 )
 HEAD_TILES = 4
 TAIL_TILES = 4
+GATHERED_SMALL = (16, 17)
 OUT_TILES = 4
 POOLED_TILES = 3
 THETA = 3
 POOLED = SLAB // 4
 V_COLS, G_COLS = 160, 352
+V_ODD, G_ODD = 128, 384
+V_TAIL, G_TAIL = 64, 320
 V_SMALL = 256
-V_ALONE, ALONE = 448, 8
-GROUPED_BUFS = 3
+V_ALONE, ALONE = 512, 7
+V_EARLY, G_EARLY, EARLY = 352, 288, 5
+GROUPED_BUFS = 2
 LOADS_AHEAD = 10
 
 FLOPS = 2 * BATCH * LOCS * CH * OUT_TILES * P
@@ -79,15 +83,21 @@ def tile_selfattention3d_pb_t_kernel(
             raw[j] = rows
 
         def shares(j):
+            if j in GATHERED_SMALL:
+                return V_TAIL, V_TAIL + G_TAIL
             if X_TILES[j][2] == 1:
                 return V_SMALL, V_SMALL
+            if j <= EARLY:
+                return V_EARLY, V_EARLY + G_EARLY
             if j <= ALONE:
                 return V_ALONE, V_ALONE
+            if j % 2:
+                return V_ODD, V_ODD + G_ODD
             return V_COLS, V_COLS + G_COLS
 
         def start_regroup(j):
             chunks = X_TILES[j][2]
-            pool = small_pool if chunks == 1 else grouped_pool
+            pool = small_pool if chunks == 1 and j not in GATHERED_SMALL else grouped_pool
             quads = pool.tile([P, chunks * CHUNK, PACK], BF16, align_bytes=64)
             grouped[j] = quads
             v_end, g_end = shares(j)
@@ -322,22 +332,21 @@ def tile_selfattention3d_pb_t_kernel(
         store_theta(0)
         convolve(1, THETA, psum_theta)
         activate_theta(1)
-        regroup_scalar(6)
         max_pool(1)
         activate_phi(0, 0, 2)
         quantise(4)
+        start_regroup(6)
+        regroup_scalar(6)
         regroup_vector(5)
         quantise(5)
+        start_regroup(7)
         pooled_matmuls(2)
         regroup_vector(6)
 
         tail = len(X_TILES) - TAIL_TILES
         to_quantise = [[], [], *[[j] for j in range(6, tail)]]
         to_quantise += [[tail, tail + 1], [tail + 2, tail + 3]]
-        to_load, to_start = LOADS_AHEAD, HEAD_TILES + GROUPED_BUFS
-        for j in range(2):
-            start_regroup(to_start)
-            to_start += 1
+        to_load, to_start = LOADS_AHEAD, HEAD_TILES + 2 * GROUPED_BUFS
         for j in range(4):
             load(to_load)
             to_load += 1

@@ -29,7 +29,7 @@ X_TILES = (
 )
 HEAD_TILES = 4
 TAIL_TILES = 4
-GATHERED_SMALL = (16, 17)
+GATHERED_SMALL = (16, 17, 18, 19)
 OUT_TILES = 4
 POOLED_TILES = 3
 THETA = 3
@@ -38,8 +38,8 @@ V_COLS, G_COLS = 160, 352
 V_ODD, G_ODD = 128, 384
 V_TAIL, G_TAIL = 64, 320
 V_SMALL = 256
-V_ALONE, ALONE = 512, 7
-V_EARLY, G_EARLY, EARLY = 352, 288, 5
+V_ALONE, ALONE = 416, 7
+V_EARLY, G_EARLY, EARLY = 288, 288, 5
 GROUPED_BUFS = 2
 LOADS_AHEAD = 10
 
@@ -84,7 +84,8 @@ def tile_selfattention3d_pb_t_kernel(
 
         def shares(j):
             if j in GATHERED_SMALL:
-                return V_TAIL, V_TAIL + G_TAIL
+                v_end = V_TAIL if j < 18 else 0
+                return v_end, v_end + G_TAIL
             if X_TILES[j][2] == 1:
                 return V_SMALL, V_SMALL
             if j <= EARLY:
@@ -119,6 +120,8 @@ def tile_selfattention3d_pb_t_kernel(
 
         def regroup_vector(j):
             end = shares(j)[0] // 4
+            if end == 0:
+                return
             dst, src = in_runs_of_four(j)
             nc.vector.tensor_copy(out=dst[:, :end], in_=src[:, :end])
 
@@ -259,9 +262,13 @@ def tile_selfattention3d_pb_t_kernel(
                 out=g_bias_row[0:1, r, :], in_=b_g.rearrange("(h c) -> h c", h=1)
             )
         w_rows = consts.tile([P, OUT_TILES, CH], BF16)
-        for o, rows in enumerate((w_phi, w_g[:P, :], w_g[P:, :], w_theta)):
+        for o, rows in ((0, w_phi), (1, w_g[:P, :])):
             nc.sync.dma_start(out=w_rows[:, o, :], in_=rows)
-        for j in range(LOADS_AHEAD):
+        load(0)
+        load(1)
+        for o, rows in ((2, w_g[P:, :]), (THETA, w_theta)):
+            nc.sync.dma_start(out=w_rows[:, o, :], in_=rows)
+        for j in range(2, LOADS_AHEAD):
             load(j)
 
         ident_bf = consts.tile([P, P], BF16)
@@ -272,7 +279,7 @@ def tile_selfattention3d_pb_t_kernel(
         w_scales = consts.tile([P, PASSES, OUT_TILES * P], U8, align_bytes=64)
         w_words = w_rows[:].bitcast(F32)
         w_grouped_words = w_grouped[:].bitcast(F32)
-        for o in range(OUT_TILES):
+        def regroup_weights(o):
             w_t = psum_tr.tile([P, PASSES, 2, P], F32, tag="tr")
             for g in range(PASSES):
                 for u in range(2):
@@ -289,23 +296,29 @@ def tile_selfattention3d_pb_t_kernel(
             else:
                 nc.scalar.copy(out=dst, in_=src)
 
-        def quantise_weights(g):
-            nc.vector.quantize_mx(
-                out=w_codes[:, g, :].bitcast(FP8X4),
-                scales=w_scales[:, g, :],
-                in_=w_grouped[:, g, :, :].rearrange("p r t -> p (r t)"),
-            )
+        def quantise_weights(o0):
+            outs = slice(o0 * P, (o0 + 2) * P)
+            for g in range(PASSES):
+                nc.vector.quantize_mx(
+                    out=w_codes[:, g, outs].bitcast(FP8X4),
+                    scales=w_scales[:, g, outs],
+                    in_=w_grouped[:, g, outs, :].rearrange("p r t -> p (r t)"),
+                )
 
-        bias_t = psum_tr.tile([P, P], BF16, tag="tr")
-        nc.tensor.transpose(bias_t[:], bias_rows[:], ident_bf[:])
+        regroup_weights(0)
+        regroup_weights(1)
         for j in range(HEAD_TILES + GROUPED_BUFS):
             start_regroup(j)
         regroup(0)
         quantise_weights(0)
         regroup(1)
-        quantise_weights(1)
         quantise(0)
         quantise(1)
+        regroup_weights(2)
+        regroup_weights(THETA)
+        bias_t = psum_tr.tile([P, P], BF16, tag="tr")
+        nc.tensor.transpose(bias_t[:], bias_rows[:], ident_bf[:])
+        quantise_weights(2)
         regroup(2)
         regroup(3)
         bias_col = consts.tile([P, OUT_TILES], F32)

@@ -34,12 +34,13 @@ OUT_TILES = 4
 POOLED_TILES = 3
 THETA = 3
 POOLED = SLAB // 4
-V_COLS, G_COLS = 160, 352
-V_ODD, G_ODD = 128, 384
-V_TAIL, G_TAIL = 64, 320
+V_COLS, G_COLS = 96, 432
+V_ODD, G_ODD = 144, 352
+V_TAIL, G_TAIL = 0, 352
 V_SMALL = 256
-V_ALONE, ALONE = 416, 7
+V_ALONE, ALONE = 352, 7
 V_EARLY, G_EARLY, EARLY = 288, 288, 5
+T_HEAD = 256
 GROUPED_BUFS = 2
 LOADS_AHEAD = 10
 
@@ -66,6 +67,7 @@ def tile_selfattention3d_pb_t_kernel(
 
         raw = {}
         grouped = {}
+        tensor_quads = {}
         x_quantised = {}
         acc = {}
         theta_act = {}
@@ -84,8 +86,7 @@ def tile_selfattention3d_pb_t_kernel(
 
         def shares(j):
             if j in GATHERED_SMALL:
-                v_end = V_TAIL if j < 18 else 0
-                return v_end, v_end + G_TAIL
+                return V_TAIL, V_TAIL + G_TAIL
             if X_TILES[j][2] == 1:
                 return V_SMALL, V_SMALL
             if j <= EARLY:
@@ -125,10 +126,28 @@ def tile_selfattention3d_pb_t_kernel(
             dst, src = in_runs_of_four(j)
             nc.vector.tensor_copy(out=dst[:, :end], in_=src[:, :end])
 
+        def regroup_tensor(j):
+            start = SLAB - T_HEAD
+            turned = psum_tr.tile([P, T_HEAD, PACK], BF16, tag="tr")
+            for n in range(0, T_HEAD, P):
+                nc.tensor.matmul(
+                    turned[:, n : n + P, :],
+                    lhsT=ident_bf[:],
+                    rhs=raw[j][:, :, start + n : start + n + P].rearrange("p t n -> p n t"),
+                    start=True,
+                    stop=True,
+                )
+            tensor_quads[j] = turned
+
         def regroup_scalar(j):
             start = shares(j)[1] // 4
+            end = X_TILES[j][2] * CHUNK // 4
             dst, src = in_runs_of_four(j)
-            nc.scalar.copy(out=dst[:, start:], in_=src[:, start:])
+            if j in tensor_quads:
+                end -= T_HEAD // 4
+            nc.scalar.copy(out=dst[:, start:end], in_=src[:, start:end])
+            if j in tensor_quads:
+                nc.scalar.copy(out=grouped[j][:, 4 * end :, :], in_=tensor_quads[j][:])
 
         def regroup(j):
             regroup_vector(j)
@@ -210,15 +229,15 @@ def tile_selfattention3d_pb_t_kernel(
             )
             phi_act[(s, u0)] = acted
 
-        def transpose_pooled(s, u0, runs):
-            g_t = psum_tr.tile([P, runs, 2, P], F32, tag="tr")
+        def transpose_pooled(s, u0, runs, pool=psum_tr, tag="tr"):
+            g_t = pool.tile([P, runs, 2, P], F32, tag=tag)
             for r in range(runs):
                 n0 = (u0 + r) * P
                 for h in range(2):
                     nc.tensor.transpose(
                         g_t[:, r, h, :], pooled[s][:, 1 + h, n0 : n0 + P], ident_f32[:]
                     )
-            phi_t = psum_tr.tile([P, runs, P], F32, tag="tr")
+            phi_t = pool.tile([P, runs, P], F32, tag=tag)
             for r in range(runs):
                 nc.tensor.transpose(phi_t[:, r, :], phi_act[(s, u0)][:, r, :], ident_f32[:])
             return phi_t, g_t
@@ -345,6 +364,8 @@ def tile_selfattention3d_pb_t_kernel(
         store_theta(0)
         convolve(1, THETA, psum_theta)
         activate_theta(1)
+        regroup_tensor(6)
+        regroup_tensor(7)
         max_pool(1)
         activate_phi(0, 0, 2)
         quantise(4)

@@ -38,9 +38,8 @@ V_COLS, G_COLS = 96, 432
 V_ODD, G_ODD = 144, 352
 V_TAIL, G_TAIL = 0, 352
 V_SMALL = 256
-V_ALONE, ALONE = 352, 7
+V_ALONE, ALONE = 416, 7
 V_EARLY, G_EARLY, EARLY = 288, 288, 5
-T_HEAD = 256
 GROUPED_BUFS = 2
 LOADS_AHEAD = 10
 
@@ -67,7 +66,6 @@ def tile_selfattention3d_pb_t_kernel(
 
         raw = {}
         grouped = {}
-        tensor_quads = {}
         x_quantised = {}
         acc = {}
         theta_act = {}
@@ -126,28 +124,10 @@ def tile_selfattention3d_pb_t_kernel(
             dst, src = in_runs_of_four(j)
             nc.vector.tensor_copy(out=dst[:, :end], in_=src[:, :end])
 
-        def regroup_tensor(j):
-            start = SLAB - T_HEAD
-            turned = psum_tr.tile([P, T_HEAD, PACK], BF16, tag="tr")
-            for n in range(0, T_HEAD, P):
-                nc.tensor.matmul(
-                    turned[:, n : n + P, :],
-                    lhsT=ident_bf[:],
-                    rhs=raw[j][:, :, start + n : start + n + P].rearrange("p t n -> p n t"),
-                    start=True,
-                    stop=True,
-                )
-            tensor_quads[j] = turned
-
         def regroup_scalar(j):
             start = shares(j)[1] // 4
-            end = X_TILES[j][2] * CHUNK // 4
             dst, src = in_runs_of_four(j)
-            if j in tensor_quads:
-                end -= T_HEAD // 4
-            nc.scalar.copy(out=dst[:, start:end], in_=src[:, start:end])
-            if j in tensor_quads:
-                nc.scalar.copy(out=grouped[j][:, 4 * end :, :], in_=tensor_quads[j][:])
+            nc.scalar.copy(out=dst[:, start:], in_=src[:, start:])
 
         def regroup(j):
             regroup_vector(j)
@@ -229,15 +209,15 @@ def tile_selfattention3d_pb_t_kernel(
             )
             phi_act[(s, u0)] = acted
 
-        def transpose_pooled(s, u0, runs, pool=psum_tr, tag="tr"):
-            g_t = pool.tile([P, runs, 2, P], F32, tag=tag)
+        def transpose_pooled(s, u0, runs):
+            g_t = psum_tr.tile([P, runs, 2, P], F32, tag="tr")
             for r in range(runs):
                 n0 = (u0 + r) * P
                 for h in range(2):
                     nc.tensor.transpose(
                         g_t[:, r, h, :], pooled[s][:, 1 + h, n0 : n0 + P], ident_f32[:]
                     )
-            phi_t = pool.tile([P, runs, P], F32, tag=tag)
+            phi_t = psum_tr.tile([P, runs, P], F32, tag="tr")
             for r in range(runs):
                 nc.tensor.transpose(phi_t[:, r, :], phi_act[(s, u0)][:, r, :], ident_f32[:])
             return phi_t, g_t
@@ -364,8 +344,6 @@ def tile_selfattention3d_pb_t_kernel(
         store_theta(0)
         convolve(1, THETA, psum_theta)
         activate_theta(1)
-        regroup_tensor(6)
-        regroup_tensor(7)
         max_pool(1)
         activate_phi(0, 0, 2)
         quantise(4)
@@ -426,6 +404,7 @@ def tile_selfattention3d_pb_t_kernel(
         max_pool(LAST - 1)
         store_theta(LAST - 2)
         transposed = transpose_pooled(s - 1, 0, 2)
+        store_theta(LAST - 1, pool=psum_pooled, tag="sums")
         convolve(LAST, 0, psum_pooled)
         activate_phi(s, 0, 1)
         convolve(LAST, THETA, psum_theta)
@@ -434,7 +413,6 @@ def tile_selfattention3d_pb_t_kernel(
             convolve(LAST, o, psum_pooled)
         store_pooled(s - 1, 0, 2, *transposed)
         max_pool(LAST)
-        store_theta(LAST - 1, nc.vector.tensor_copy, pool=psum_pooled, tag="sums")
         activate_phi(s, 1, 1)
         transposed = transpose_pooled(s, 0, 1)
         store_pooled(s, 0, 1, *transposed)

from contextlib import ExitStack

import concourse.mybir as mybir
from concourse.masks import make_identity

BF16 = mybir.dt.bfloat16
F32 = mybir.dt.float32
U32 = mybir.dt.uint32
U8 = mybir.dt.uint8
FP8X4 = mybir.dt.float8_e4m3fn_x4
ACT = mybir.ActivationFunctionType

P = 128
PACK = 4
K_PASS = P * PACK
BATCH = 2
CH = 1024
PASSES = CH // K_PASS
LOCS = 16 * 16 * 16
CHUNK = 512
SLAB = 2 * CHUNK
SLABS_PER_BATCH = LOCS // SLAB
CHUNKS = BATCH * LOCS // CHUNK
LAST = CHUNKS - 1
X_TILES = (
    [(g, h, 1) for h in range(2) for g in range(PASSES)]
    + [(g, h, 2) for h in range(2, CHUNKS - 2, 2) for g in range(PASSES)]
    + [(g, h, 1) for h in (LAST - 1, LAST) for g in range(PASSES)]
)
HEAD_TILES = 4
TAIL_TILES = 4
GATHERED_SMALL = (16, 17, 18, 19)
OUT_TILES = 4
POOLED_TILES = 3
THETA = 3
POOLED = SLAB // 4
V_COLS, G_COLS = 96, 432
V_ODD, G_ODD = 144, 352
V_TAIL, G_TAIL = 0, 352
V_SMALL = 256
V_ALONE, ALONE = 416, 7
V_EARLY, G_EARLY, EARLY = 288, 288, 5
GROUPED_BUFS = 2
LOADS_AHEAD = 10

FLOPS = 2 * BATCH * LOCS * CH * OUT_TILES * P


def tile_selfattention3d_pb_t_kernel(
    tc, x, w_theta, b_theta, w_phi, b_phi, w_g, b_g, out_0, out_1, out_2
):
    nc = tc.nc
    x_view = x.rearrange("b (g p t) f i j -> b g p t (f i j)", g=PASSES, t=PACK, p=P)

    with ExitStack() as ctx:
        consts = ctx.enter_context(tc.tile_pool(name="consts", bufs=1))
        raw_pool = ctx.enter_context(tc.tile_pool(name="raw", bufs=LOADS_AHEAD))
        grouped_pool = ctx.enter_context(tc.tile_pool(name="grouped", bufs=GROUPED_BUFS))
        small_pool = ctx.enter_context(tc.tile_pool(name="small", bufs=4))
        mx_pool = ctx.enter_context(tc.tile_pool(name="mx", bufs=6))
        work = ctx.enter_context(tc.tile_pool(name="work", bufs=3))
        out_pool = ctx.enter_context(tc.tile_pool(name="out", bufs=6))
        psum_pooled = ctx.enter_context(tc.psum_pool(name="psum_pooled", bufs=4))
        psum_theta = ctx.enter_context(tc.psum_pool(name="psum_theta", bufs=1))
        psum_tr = ctx.enter_context(tc.psum_pool(name="psum_tr", bufs=3))

        raw = {}
        grouped = {}
        x_quantised = {}
        acc = {}
        theta_act = {}
        pooled = {}
        phi_act = {}

        def load(j):
            if j >= len(X_TILES):
                return
            g, h, chunks = X_TILES[j]
            bt, n0 = divmod(h * CHUNK, LOCS)
            width = chunks * CHUNK
            rows = raw_pool.tile([P, PACK, width], BF16)
            nc.sync.dma_start(out=rows[:], in_=x_view[bt, g, :, :, n0 : n0 + width])
            raw[j] = rows

        def shares(j):
            if j in GATHERED_SMALL:
                return V_TAIL, V_TAIL + G_TAIL
            if X_TILES[j][2] == 1:
                return V_SMALL, V_SMALL
            if j <= EARLY:
                return V_EARLY, V_EARLY + G_EARLY
            if j <= ALONE:
                return V_ALONE, V_ALONE
            if j % 2:
                return V_ODD, V_ODD + G_ODD
            return V_COLS, V_COLS + G_COLS

        def start_regroup(j):
            chunks = X_TILES[j][2]
            pool = small_pool if chunks == 1 and j not in GATHERED_SMALL else grouped_pool
            quads = pool.tile([P, chunks * CHUNK, PACK], BF16, align_bytes=64)
            grouped[j] = quads
            v_end, g_end = shares(j)
            if g_end == v_end:
                return
            nc.gpsimd.tensor_scalar(
                out=quads[:, v_end:g_end, :],
                in0=raw[j][:, :, v_end:g_end].rearrange("p t n -> p n t"),
                scalar1=1.0,
                scalar2=0.0,
                op0=mybir.AluOpType.mult,
                op1=mybir.AluOpType.add,
            )

        def in_runs_of_four(j):
            dst = grouped[j][:].rearrange("p (c i) t -> p c t i", i=4)
            src = raw[j][:].rearrange("p t (c i) -> p c t i", i=4)
            return dst, src

        def regroup_vector(j):
            end = shares(j)[0] // 4
            if end == 0:
                return
            dst, src = in_runs_of_four(j)
            nc.vector.tensor_copy(out=dst[:, :end], in_=src[:, :end])

        def regroup_scalar(j):
            start = shares(j)[1] // 4
            dst, src = in_runs_of_four(j)
            nc.scalar.copy(out=dst[:, start:], in_=src[:, start:])

        def regroup(j):
            regroup_vector(j)
            regroup_scalar(j)

        def quantise(j):
            g, h, chunks = X_TILES[j]
            width = chunks * CHUNK
            codes = mx_pool.tile([P, width], U32, align_bytes=64)
            scales = mx_pool.tile([P, width], U8, align_bytes=64)
            nc.vector.quantize_mx(
                out=codes[:].bitcast(FP8X4),
                scales=scales[:],
                in_=grouped[j][:].rearrange("p n t -> p (n t)"),
            )
            for c in range(chunks):
                cols = slice(c * CHUNK, (c + 1) * CHUNK)
                x_quantised[(g, h + c)] = (codes[:, cols], scales[:, cols])

        def convolve(h, o, pool):
            outs = slice(o * P, (o + 1) * P)
            sums = pool.tile([P, CHUNK], F32)
            for g in range(PASSES):
                codes, scales = x_quantised[(g, h)]
                nc.tensor.matmul_mx(
                    out=sums[:],
                    lhsT=w_codes[:, g, outs].bitcast(FP8X4),
                    lhsT_scale=w_scales[:, g, outs],
                    rhs=codes.bitcast(FP8X4),
                    rhs_scale=scales,
                    start=(g == 0),
                    stop=(g == PASSES - 1),
                )
            acc[(h, o)] = sums

        def max_pool(h):
            s, u = divmod(h, 2)
            if u == 0:
                pooled[s] = work.tile([P, POOLED_TILES, POOLED], F32, name="pooled_max")
            for o in range(POOLED_TILES):
                nc.vector.tensor_reduce(
                    out=pooled[s][:, o, u * P : (u + 1) * P].rearrange("p (r j) -> p r j", j=8),
                    in_=acc[(h, o)][:].rearrange("p (r a j b) -> p r j a b", a=2, j=8, b=2),
                    axis=mybir.AxisListType.XY,
                    op=mybir.AluOpType.max,
                )

        def activate_theta(h):
            th = work.tile([P, 4, P], F32, name="th")
            nc.scalar.activation(
                out=th[:],
                in_=acc[(h, THETA)][:].rearrange("p (q r) -> p r q", r=4),
                func=ACT.Tanh,
                bias=bias_col[:, THETA : THETA + 1],
            )
            theta_act[h] = th

        def store_theta(h, copy=nc.scalar.copy, pool=psum_tr, tag="tr"):
            bt, n0 = divmod(h * CHUNK, LOCS)
            th_t = pool.tile([P, 4, P], F32, tag=tag)
            for r in range(4):
                nc.tensor.transpose(th_t[:, r, :], theta_act[h][:, r, :], ident_f32[:])
            th_out = out_pool.tile([P, 4, P], F32)
            copy(out=th_out[:], in_=th_t[:])
            nc.sync.dma_start(
                out=out_0[bt, n0 : n0 + CHUNK, :].rearrange("(q r) c -> q r c", r=4),
                in_=th_out[:],
            )

        def activate_phi(s, u0, runs):
            acted = work.tile([P, runs, P], F32, name="phi_acted")
            nc.scalar.activation(
                out=acted[:],
                in_=pooled[s][:, 0, u0 * P : (u0 + runs) * P].rearrange(
                    "p (q r) -> p r q", r=runs
                ),
                func=ACT.Tanh,
                bias=bias_col[:, 0:1],
            )
            phi_act[(s, u0)] = acted

        def transpose_pooled(s, u0, runs):
            g_t = psum_tr.tile([P, runs, 2, P], F32, tag="tr")
            for r in range(runs):
                n0 = (u0 + r) * P
                for h in range(2):
                    nc.tensor.transpose(
                        g_t[:, r, h, :], pooled[s][:, 1 + h, n0 : n0 + P], ident_f32[:]
                    )
            phi_t = psum_tr.tile([P, runs, P], F32, tag="tr")
            for r in range(runs):
                nc.tensor.transpose(phi_t[:, r, :], phi_act[(s, u0)][:, r, :], ident_f32[:])
            return phi_t, g_t

        def store_pooled(s, u0, runs, phi_t, g_t, gpsimd_adds=False):
            bt = s // SLABS_PER_BATCH
            m0 = (s % SLABS_PER_BATCH) * POOLED + u0 * P
            m1 = m0 + runs * P
            g_out = out_pool.tile([P, runs, 2 * P], F32)
            g_rows = g_t[:].rearrange("p r h c -> p r (h c)")
            if gpsimd_adds:
                nc.scalar.copy(out=g_out[:], in_=g_rows)
                nc.gpsimd.tensor_add(out=g_out[:], in0=g_out[:], in1=g_bias[:, :runs, :])
            else:
                nc.vector.tensor_add(out=g_out[:], in0=g_rows, in1=g_bias[:, :runs, :])
            nc.sync.dma_start(
                out=out_2[bt, m0:m1, :].rearrange("(r q) c -> q r c", r=runs), in_=g_out[:]
            )
            phi_out = out_pool.tile([P, runs, P], F32)
            nc.scalar.copy(out=phi_out[:], in_=phi_t[:])
            nc.sync.dma_start(
                out=out_1[bt, m0:m1, :].rearrange("(q r) c -> q r c", r=runs), in_=phi_out[:]
            )

        ctx.enter_context(tc.manual_schedule())

        ident_f32 = consts.tile([P, P], F32)
        make_identity(nc, ident_f32[:])
        bias_rows = consts.tile([P, P], BF16)
        nc.vector.memset(bias_rows[:], 0.0)
        g_bias_row = consts.tile([P, 2, 2 * P], BF16)
        nc.vector.memset(g_bias_row[:], 0.0)
        ones = consts.tile([P, P], BF16)
        nc.vector.memset(ones[:], 1.0)
        nc.scalar.dma_start(out=bias_rows[0:1, :], in_=b_phi.rearrange("(h c) -> h c", h=1))
        nc.scalar.dma_start(
            out=bias_rows[THETA : THETA + 1, :], in_=b_theta.rearrange("(h c) -> h c", h=1)
        )
        for r in range(2):
            nc.scalar.dma_start(
                out=g_bias_row[0:1, r, :], in_=b_g.rearrange("(h c) -> h c", h=1)
            )
        w_rows = consts.tile([P, OUT_TILES, CH], BF16)
        for o, rows in ((0, w_phi), (1, w_g[:P, :])):
            nc.sync.dma_start(out=w_rows[:, o, :], in_=rows)
        load(0)
        load(1)
        for o, rows in ((2, w_g[P:, :]), (THETA, w_theta)):
            nc.sync.dma_start(out=w_rows[:, o, :], in_=rows)
        for j in range(2, LOADS_AHEAD):
            load(j)

        ident_bf = consts.tile([P, P], BF16)
        make_identity(nc, ident_bf[:])

        w_grouped = consts.tile([P, PASSES, OUT_TILES * P, PACK], BF16, align_bytes=64)
        w_codes = consts.tile([P, PASSES, OUT_TILES * P], U32, align_bytes=64)
        w_scales = consts.tile([P, PASSES, OUT_TILES * P], U8, align_bytes=64)
        w_words = w_rows[:].bitcast(F32)
        w_grouped_words = w_grouped[:].bitcast(F32)
        def regroup_weights(o):
            w_t = psum_tr.tile([P, PASSES, 2, P], F32, tag="tr")
            for g in range(PASSES):
                for u in range(2):
                    w0 = g * (K_PASS // 2)
                    nc.tensor.transpose(
                        w_t[:, g, u, :],
                        w_words[:, o, w0 + u : w0 + K_PASS // 2 : 2],
                        ident_f32[:],
                    )
            dst = w_grouped_words[:, :, o * P : (o + 1) * P, :]
            src = w_t[:].rearrange("p g u r -> p g r u")
            if o % 2 == 0:
                nc.vector.tensor_copy(out=dst, in_=src)
            else:
                nc.scalar.copy(out=dst, in_=src)

        def quantise_weights(o0):
            outs = slice(o0 * P, (o0 + 2) * P)
            for g in range(PASSES):
                nc.vector.quantize_mx(
                    out=w_codes[:, g, outs].bitcast(FP8X4),
                    scales=w_scales[:, g, outs],
                    in_=w_grouped[:, g, outs, :].rearrange("p r t -> p (r t)"),
                )

        regroup_weights(0)
        regroup_weights(1)
        for j in range(HEAD_TILES + GROUPED_BUFS):
            start_regroup(j)
        regroup(0)
        quantise_weights(0)
        regroup(1)
        quantise(0)
        quantise(1)
        regroup_weights(2)
        regroup_weights(THETA)
        bias_t = psum_tr.tile([P, P], BF16, tag="tr")
        nc.tensor.transpose(bias_t[:], bias_rows[:], ident_bf[:])
        quantise_weights(2)
        regroup(2)
        regroup(3)
        bias_col = consts.tile([P, OUT_TILES], F32)
        nc.vector.tensor_copy(out=bias_col[:], in_=bias_t[:, 0:OUT_TILES])

        def pooled_matmuls(h):
            for o in range(POOLED_TILES):
                convolve(h, o, psum_pooled)

        pooled_matmuls(0)
        g_bias_t = psum_tr.tile([P, 2, 2 * P], F32, tag="tr")
        nc.tensor.matmul(g_bias_t[:], lhsT=ones[:], rhs=g_bias_row[:], start=True, stop=True)
        quantise(2)
        quantise(3)
        convolve(0, THETA, psum_theta)
        regroup_scalar(4)
        activate_theta(0)
        g_bias = consts.tile([P, 2, 2 * P], F32)
        nc.scalar.copy(out=g_bias[:], in_=g_bias_t[:])
        max_pool(0)
        pooled_matmuls(1)
        regroup_vector(4)
        regroup_scalar(5)
        store_theta(0)
        convolve(1, THETA, psum_theta)
        activate_theta(1)
        max_pool(1)
        activate_phi(0, 0, 2)
        quantise(4)
        start_regroup(6)
        regroup_scalar(6)
        regroup_vector(5)
        quantise(5)
        start_regroup(7)
        pooled_matmuls(2)
        regroup_vector(6)

        tail = len(X_TILES) - TAIL_TILES
        to_quantise = [[], [], *[[j] for j in range(6, tail)]]
        to_quantise += [[tail, tail + 1], [tail + 2, tail + 3]]
        to_load, to_start = LOADS_AHEAD, HEAD_TILES + 2 * GROUPED_BUFS
        for j in range(4):
            load(to_load)
            to_load += 1
        for h in range(2, LAST - 2):
            for j in to_quantise[h]:
                load(to_load)
                to_load += 1
                quantise(j)
                if to_start < len(X_TILES):
                    start_regroup(to_start)
                    to_start += 1
            for j in to_quantise[h + 1]:
                while to_start <= j:
                    start_regroup(to_start)
                    to_start += 1
                regroup(j)
            convolve(h, THETA, psum_theta)
            activate_theta(h)
            store_theta(h - 1)
            slab_done = h % 2 == 0
            if slab_done:
                transposed = transpose_pooled(h // 2 - 1, 0, 2)
            max_pool(h)
            if slab_done:
                store_pooled(h // 2 - 1, 0, 2, *transposed)
            if h % 2 == 1:
                activate_phi(h // 2, 0, 2)
            pooled_matmuls(h + 1)

        s = LAST // 2
        convolve(LAST - 2, THETA, psum_theta)
        activate_theta(LAST - 2)
        store_theta(LAST - 3)
        max_pool(LAST - 2)
        activate_phi(s - 1, 0, 2)
        for j in to_quantise[LAST - 2]:
            quantise(j)
        convolve(LAST - 1, 0, psum_pooled)
        convolve(LAST - 1, 1, psum_pooled)
        convolve(LAST - 1, THETA, psum_theta)
        activate_theta(LAST - 1)
        convolve(LAST - 1, 2, psum_pooled)
        max_pool(LAST - 1)
        store_theta(LAST - 2)
        transposed = transpose_pooled(s - 1, 0, 2)
        store_theta(LAST - 1, pool=psum_pooled, tag="sums")
        convolve(LAST, 0, psum_pooled)
        activate_phi(s, 0, 1)
        convolve(LAST, THETA, psum_theta)
        activate_theta(LAST)
        for o in range(1, POOLED_TILES):
            convolve(LAST, o, psum_pooled)
        store_pooled(s - 1, 0, 2, *transposed)
        max_pool(LAST)
        activate_phi(s, 1, 1)
        transposed = transpose_pooled(s, 0, 1)
        store_pooled(s, 0, 1, *transposed)
        store_theta(LAST, pool=psum_pooled, tag="sums")
        store_pooled(s, 1, 1, *transpose_pooled(s, 1, 1))
